import numpy as np
import ml_dtypes


def mxq(x, axis, fmt="e4m3"):
    dtype, down = {"e4m3": (ml_dtypes.float8_e4m3fn, 7), "e5m2": (ml_dtypes.float8_e5m2, 14)}[fmt]
    v = np.moveaxis(np.asarray(x, np.float32).astype(ml_dtypes.bfloat16).astype(np.float64), axis, -1)
    blocks = v.reshape(v.shape[:-1] + (-1, 32))
    amax = np.abs(blocks).max(-1, keepdims=True)
    byte = np.maximum(np.where(amax > 0, np.frexp(amax)[1] - 1 + 127, 0) - down, 1)
    scale = np.exp2(byte - 127.0)
    codes = (blocks / scale).astype(np.float32).astype(dtype).astype(np.float64)
    return np.moveaxis((codes * scale).reshape(v.shape), -1, axis)


WIDE = False


def mx_kscale(k):
    if not WIDE:
        return np.ones(k)
    levels = np.array([10, -10, 5, -5, 0])
    if k % 512:
        return np.exp2(np.random.permutation(np.resize(levels, k // 32))).repeat(32)
    a = np.empty((k // 512, 16))
    for p in range(k // 512):
        a[p, :8] = np.random.permutation(np.resize(levels, 8))
        for g in range(8):
            far = levels[np.abs(levels - a[p, g]) >= 10]
            a[p, g + 8] = far[np.random.randint(len(far))]
    return np.exp2(a.ravel()).repeat(32)


BF16 = ml_dtypes.bfloat16


def bf(x):
    return np.asarray(x, np.float32).astype(BF16)


def f64(x):
    return np.asarray(x).astype(np.float64)


S, B, D, H, F = 512, 2, 1024, 2, 2048
HD = D // H
EPS = 1e-8
ZMAX = 6.0
NTERMS = 120


def rmsnorm(x, w):
    ms = np.mean(x * x, axis=-1, keepdims=True)
    return w * (x / np.sqrt(ms + EPS))


def erf(z):
    a = np.clip(z, -ZMAX, ZMAX)
    y = 2.0 * a * a
    term = a.copy()
    tot = a.copy()
    for n in range(1, NTERMS):
        term *= y
        term *= 1.0 / (2 * n + 1)
        tot += term
    return 2.0 / np.sqrt(np.pi) * np.exp(-a * a) * tot


def gelu_erf(v):
    return 0.5 * v * (1.0 + erf(v / np.sqrt(2.0)))


def setup_inputs():
    s, t = mx_kscale(D), mx_kscale(D)
    return {"h_attn": bf(np.random.standard_normal((B, H, S, HD)) * 0.35 * s.reshape(H, 1, HD)),
            "x": bf(np.random.standard_normal((S, B, D))),
            "out_proj_w": bf(np.random.standard_normal((D, D)) * 2.0 / np.sqrt(D) / s[None, :]),
            "out_proj_b": bf(np.random.standard_normal(D) * 0.2),
            "w_norm2": bf((1.0 + 0.1 * np.random.standard_normal(D)) * t),
            "W1": bf(np.random.standard_normal((F, D)) / np.sqrt(D) / t[None, :]),
            "b1": bf(np.random.standard_normal(F) * 0.3)}


def reference(h_attn, x, out_proj_w, out_proj_b, w_norm2, W1, b1):
    c = f64(h_attn).transpose(2, 0, 1, 3).reshape(S, B, D)
    attn_out = (mxq(c, 2, "e4m3") @ mxq(f64(out_proj_w), 1, "e4m3").T) + f64(out_proj_b)
    x1 = f64(x) + attn_out
    m = rmsnorm(x1, f64(w_norm2))
    g = gelu_erf((mxq(m, 2, "e4m3") @ mxq(f64(W1), 1, "e4m3").T) + f64(b1))
    return x1, g

@@ -1,0 +1,359 @@
+from contextlib import ExitStack
+
+import concourse.mybir as mybir
+from concourse.masks import make_identity
+
+BF16 = mybir.dt.bfloat16
+F32 = mybir.dt.float32
+U32 = mybir.dt.uint32
+U8 = mybir.dt.uint8
+FP8X4 = mybir.dt.float8_e4m3fn_x4
+ALU = mybir.AluOpType
+ACT = mybir.ActivationFunctionType
+
+P = 128
+PACK = 4
+K_PASS = P * PACK
+BANK = 512
+SEQ, BATCH, DIM, HEADS, FF = 512, 2, 1024, 2, 2048
+HEAD_DIM = DIM // HEADS
+PASSES = DIM // K_PASS
+POS = SEQ // P
+TILES = BATCH * POS
+PAIRS = K_PASS // 2
+HALVES = PAIRS // P
+EPS = 1e-8
+BO_ROWS, W2_ROWS, B1_ROWS = DIM // BANK, DIM // BANK, FF // BANK
+UNITS_PER_ROUND = 2
+
+FLOPS = 2 * SEQ * BATCH * DIM * (DIM + FF)
+
+
+def tile_transformerblock_pb_kernel(
+    tc, h_attn, x, out_proj_w, out_proj_b, w_norm2, W1, b1, out_0, out_1
+):
+    nc = tc.nc
+    with ExitStack() as stack:
+        const = stack.enter_context(tc.tile_pool(name="const", bufs=1))
+        raw = stack.enter_context(tc.tile_pool(name="raw", bufs=1))
+        keep = stack.enter_context(tc.tile_pool(name="keep", bufs=1))
+        stream = stack.enter_context(tc.tile_pool(name="stream", bufs=3))
+        psum = stack.enter_context(tc.psum_pool(name="psum", bufs=8))
+        stack.enter_context(tc.manual_schedule())
+
+        vector_rows = const.tile([P, BANK], BF16)
+        nc.vector.memset(vector_rows[:], 0.0)
+        table_warmer = const.tile([P, 1], F32)
+        nc.vector.memset(table_warmer[:], 0.0)
+        minus_half = const.tile([P, 1], F32)
+        nc.vector.memset(minus_half[:], -0.5)
+        ident_f32 = const.tile([P, P], F32)
+        make_identity(nc, ident_f32[:])
+        ident_bf16 = const.tile([P, P], BF16)
+        make_identity(nc, ident_bf16[:])
+        nc.scalar.activation(out=table_warmer[:], in_=table_warmer[:], func=ACT.Gelu)
+
+        x_view = x.rearrange("(p j) b d -> p j b d", j=POS)
+        out0_view = out_0.rearrange("(p j) b d -> p j b d", j=POS)
+        out1_view = out_1.rearrange("(p j) b f -> p j b f", j=POS)
+        c_raw = {}
+        x_raw = {}
+        wo_raw = {}
+        w1_raw = {}
+
+        def load_heads(b):
+            for head in range(HEADS):
+                c_raw[b, head] = raw.tile([P, POS * HEAD_DIM], BF16, name="c_raw_%d_%d" % (b, head))
+                nc.sync.dma_start(
+                    out=c_raw[b, head][:], in_=h_attn[b, head].rearrange("(p j) d -> p (j d)", j=POS)
+                )
+
+        def load_x(b):
+            x_raw[b] = raw.tile([P, POS * DIM], BF16, name="x_raw_%d" % b)
+            nc.sync.dma_start(out=x_raw[b][:].rearrange("p (j d) -> p j d", j=POS), in_=x_view[:, :, b, :])
+
+        def load_vector(first_row, n_rows, vector):
+            nc.sync.dma_start(
+                out=vector_rows[first_row : first_row + n_rows, :], in_=vector.rearrange("(r n) -> r n", n=BANK)
+            )
+
+        def load_weight(store, name, weight, chunk):
+            store[chunk] = raw.tile([P, PACK * DIM], BF16, name="%s_%d" % (name, chunk))
+            nc.sync.dma_start(
+                out=store[chunk][:].rearrange("p (a k) -> p a k", a=PACK),
+                in_=weight[chunk * BANK : (chunk + 1) * BANK, :].rearrange("(a p) k -> p a k", p=P),
+            )
+
+        load_heads(0)
+        load_vector(0, BO_ROWS, out_proj_b)
+        load_vector(BO_ROWS, W2_ROWS, w_norm2)
+        load_vector(BO_ROWS + W2_ROWS, B1_ROWS, b1)
+        load_x(0)
+        load_weight(wo_raw, "wo_raw", out_proj_w, 0)
+        load_weight(wo_raw, "wo_raw", out_proj_w, 1)
+        load_weight(w1_raw, "w1_raw", W1, 0)
+        load_heads(1)
+        load_x(1)
+        load_weight(w1_raw, "w1_raw", W1, 1)
+        load_weight(w1_raw, "w1_raw", W1, 2)
+        load_weight(w1_raw, "w1_raw", W1, 3)
+
+        c_words = keep.tile([P, BATCH, PASSES, POS, P], U32, align_bytes=64)
+        c_scales = keep.tile([P, BATCH, PASSES, POS, P], U8, align_bytes=64)
+        m_words = keep.tile([P, TILES, PASSES, P], U32, align_bytes=64)
+        m_scales = keep.tile([P, TILES, PASSES, P], U8, align_bytes=64)
+        wo_words = keep.tile([P, PASSES, DIM], U32, align_bytes=64)
+        wo_scales = keep.tile([P, PASSES, DIM], U8, align_bytes=64)
+        w1_words = keep.tile([P, PASSES, FF], U32, align_bytes=64)
+        w1_scales = keep.tile([P, PASSES, FF], U8, align_bytes=64)
+
+        spread = const.tile([P, BO_ROWS + W2_ROWS + B1_ROWS, BANK], BF16)
+        bo_all = spread[:, 0:BO_ROWS, :].rearrange("p r n -> p (r n)")
+        w2_all = spread[:, BO_ROWS : BO_ROWS + W2_ROWS, :].rearrange("p r n -> p (r n)")
+        b1_all = spread[:, BO_ROWS + W2_ROWS :, :].rearrange("p r n -> p (r n)")
+
+        def spread_row(row):
+            bank = psum.tile([P, BANK], F32, tag="bank")
+            nc.tensor.matmul(
+                out=bank[:],
+                lhsT=ident_bf16[:, row : row + 1].to_broadcast([P, P]),
+                rhs=vector_rows[:],
+                start=True,
+                stop=True,
+            )
+            nc.scalar.copy(out=spread[:, row, :], in_=bank[:])
+
+        def token_unit(b, g):
+            words = c_raw[b, g][:].bitcast(F32)
+            return (
+                [words[:, j * PAIRS : (j + 1) * PAIRS] for j in range(POS)],
+                c_words[:, b, g, :, :].rearrange("p j r -> p (j r)"),
+                c_scales[:, b, g, :, :].rearrange("p j r -> p (j r)"),
+            )
+
+        def weight_unit(w_raw, w_words, w_scales, chunk, g):
+            words = w_raw[chunk][:].bitcast(F32)
+            cols = slice(chunk * BANK, (chunk + 1) * BANK)
+            return (
+                [words[:, (a * PASSES + g) * PAIRS : (a * PASSES + g + 1) * PAIRS] for a in range(PACK)],
+                w_words[:, g, cols],
+                w_scales[:, g, cols],
+            )
+
+        def transpose_unit(unit):
+            blocks = unit[0]
+            banks = []
+            for half in range(2):
+                bank = psum.tile([P, 2, HALVES, P], F32, tag="bank")
+                for i in range(2):
+                    for u in range(HALVES):
+                        nc.tensor.transpose(
+                            bank[:, i, u, :], blocks[2 * half + i][:, u::HALVES], ident_f32[:]
+                        )
+                banks.append(bank)
+            return banks
+
+        def copy_out_unit(banks):
+            grouped = stream.tile([P, PACK * BANK], BF16, align_bytes=64, bufs=2 * UNITS_PER_ROUND)
+            grouped_words = grouped[:].bitcast(F32).rearrange("p (i r u) -> p i r u", i=PACK, u=HALVES)
+            for half in range(2):
+                nc.scalar.copy(
+                    out=grouped_words[:, 2 * half : 2 * half + 2, :, :],
+                    in_=banks[half][:].rearrange("p i u r -> p i r u"),
+                )
+            return grouped
+
+        def quantise_unit(unit, grouped):
+            nc.vector.quantize_mx(out=unit[1].bitcast(FP8X4), scales=unit[2], in_=grouped[:])
+
+        x1_tiles = {}
+
+        def add_bias_to_x(tile):
+            b, j = divmod(tile, POS)
+            x1_tiles[tile] = keep.tile([P, DIM], F32, name="x1_%d" % tile)
+            nc.vector.tensor_tensor(
+                out=x1_tiles[tile][:], in0=x_raw[b][:, j * DIM : (j + 1) * DIM], in1=bo_all, op=ALU.add
+            )
+
+        attn_banks = {}
+
+        def project(tile):
+            b, j = divmod(tile, POS)
+            for n in range(DIM // BANK):
+                cols = slice(n * BANK, (n + 1) * BANK)
+                attn_banks[tile, n] = psum.tile([P, BANK], F32, tag="bank", name="attn_%d_%d" % (tile, n))
+                for g in range(PASSES):
+                    nc.tensor.matmul_mx(
+                        out=attn_banks[tile, n][:],
+                        lhsT=c_words[:, b, g, j, :].bitcast(FP8X4),
+                        lhsT_scale=c_scales[:, b, g, j, :],
+                        rhs=wo_words[:, g, cols].bitcast(FP8X4),
+                        rhs_scale=wo_scales[:, g, cols],
+                        start=(g == 0),
+                        stop=(g == PASSES - 1),
+                    )
+
+        def add_residual(tile):
+            b, j = divmod(tile, POS)
+            x1 = x1_tiles[tile]
+            for n in range(DIM // BANK):
+                cols = slice(n * BANK, (n + 1) * BANK)
+                nc.vector.tensor_tensor(out=x1[:, cols], in0=attn_banks[tile, n][:], in1=x1[:, cols], op=ALU.add)
+            nc.sync.dma_start(out=out0_view[:, j, b, :], in_=x1[:])
+
+        mean_sq = const.tile([P, TILES], F32)
+        mean_sq_eps = const.tile([P, TILES], F32)
+        inv_rms = const.tile([P, TILES], F32)
+
+        def inverse_rms(tile):
+            col = slice(tile, tile + 1)
+            squares = stream.tile([P, DIM], BF16, bufs=2)
+            nc.scalar.activation(
+                out=squares[:], in_=x1_tiles[tile][:], func=ACT.Square, scale=DIM**-0.5, accum_out=mean_sq[:, col]
+            )
+            nc.gpsimd.tensor_scalar(
+                out=mean_sq_eps[:, col], in0=mean_sq[:, col], scalar1=EPS, scalar2=1.0, op0=ALU.add, op1=ALU.mult
+            )
+            nc.gpsimd.tensor_tensor(out=inv_rms[:, col], in0=mean_sq_eps[:, col], in1=minus_half[:], op=ALU.pow)
+
+        m_tiles = {}
+
+        def normalise(tile):
+            m_tiles[tile] = stream.tile([P, PACK, DIM // PACK], BF16, name="m_%d" % tile, tag="m")
+            x1_planes = x1_tiles[tile][:].rearrange("p (w t) -> p t w", t=PACK)
+            w2_planes = w2_all.rearrange("p (w t) -> p t w", t=PACK)
+            for e in range(2):
+                planes = slice(2 * e, 2 * e + 2)
+                nc.vector.scalar_tensor_tensor(
+                    out=m_tiles[tile][:, planes, :],
+                    in0=x1_planes[:, planes, :],
+                    scalar=inv_rms[:, tile : tile + 1],
+                    in1=w2_planes[:, planes, :],
+                    op0=ALU.mult,
+                    op1=ALU.mult,
+                )
+
+        m_banks = {}
+
+        def transpose_m(tile):
+            m_banks[tile] = psum.tile([P, PASSES, PACK, P], BF16, tag="bank", name="m_bank_%d" % tile)
+            for g in range(PASSES):
+                for t in range(PACK):
+                    nc.tensor.transpose(
+                        m_banks[tile][:, g, t, :], m_tiles[tile][:, t, g * P : (g + 1) * P], ident_bf16[:]
+                    )
+
+        grouped_m = {}
+
+        def copy_out_m(tile):
+            grouped_m[tile] = stream.tile(
+                [P, PASSES * P * PACK], BF16, align_bytes=64, name="grouped_m_%d" % tile, tag="grouped_m"
+            )
+            nc.scalar.copy(
+                out=grouped_m[tile][:].rearrange("p (g r v) -> p g r v", g=PASSES, v=PACK),
+                in_=m_banks[tile][:].rearrange("p g v r -> p g r v"),
+            )
+
+        def quantise_m(tile):
+            nc.vector.quantize_mx(
+                out=m_words[:, tile, :, :].rearrange("p g r -> p (g r)").bitcast(FP8X4),
+                scales=m_scales[:, tile, :, :].rearrange("p g r -> p (g r)"),
+                in_=grouped_m[tile][:],
+            )
+
+        up_banks = {}
+
+        def up_project(tile):
+            for n in range(FF // BANK):
+                cols = slice(n * BANK, (n + 1) * BANK)
+                up_banks[tile, n] = psum.tile([P, BANK], F32, tag="bank", name="up_%d_%d" % (tile, n))
+                for g in range(PASSES):
+                    nc.tensor.matmul_mx(
+                        out=up_banks[tile, n][:],
+                        lhsT=m_words[:, tile, g, :].bitcast(FP8X4),
+                        lhsT_scale=m_scales[:, tile, g, :],
+                        rhs=w1_words[:, g, cols].bitcast(FP8X4),
+                        rhs_scale=w1_scales[:, g, cols],
+                        start=(g == 0),
+                        stop=(g == PASSES - 1),
+                    )
+
+        g_tiles = {}
+
+        def add_b1(tile):
+            g_tiles[tile] = stream.tile([P, FF], F32, name="g_%d" % tile, tag="g")
+            for n in range(FF // BANK):
+                cols = slice(n * BANK, (n + 1) * BANK)
+                nc.vector.tensor_tensor(
+                    out=g_tiles[tile][:, cols], in0=up_banks[tile, n][:], in1=b1_all[:, cols], op=ALU.add
+                )
+
+        def gelu_and_store(tile, half):
+            b, j = divmod(tile, POS)
+            for n in (2 * half, 2 * half + 1):
+                cols = slice(n * BANK, (n + 1) * BANK)
+                nc.scalar.activation(out=g_tiles[tile][:, cols], in_=g_tiles[tile][:, cols], func=ACT.Gelu)
+            cols = slice(half * FF // 2, (half + 1) * FF // 2)
+            nc.sync.dma_start(out=out1_view[:, j, b, cols], in_=g_tiles[tile][:, cols])
+
+        token_units = [token_unit(0, g) for g in range(PASSES)]
+        token_grouped = [copy_out_unit(transpose_unit(unit)) for unit in token_units]
+        for row in range(BO_ROWS + W2_ROWS):
+            spread_row(row)
+        for unit, grouped in zip(token_units, token_grouped):
+            quantise_unit(unit, grouped)
+        wo_units = [weight_unit(wo_raw, wo_words, wo_scales, chunk, g) for chunk in range(2) for g in range(PASSES)]
+        wo_grouped = []
+        for i in range(len(wo_units)):
+            wo_grouped.append(copy_out_unit(transpose_unit(wo_units[i])))
+            add_bias_to_x(i)
+            if i > 0:
+                quantise_unit(wo_units[i - 1], wo_grouped[i - 1])
+        quantise_unit(wo_units[-1], wo_grouped[-1])
+        project(0)
+
+        units = [weight_unit(w1_raw, w1_words, w1_scales, 0, g) for g in range(PASSES)]
+        units += [token_unit(1, g) for g in range(PASSES)]
+        units += [weight_unit(w1_raw, w1_words, w1_scales, chunk, g) for chunk in (1, 2, 3) for g in range(PASSES)]
+        unit_rounds = (len(units) + UNITS_PER_ROUND - 1) // UNITS_PER_ROUND
+        first_up_round = unit_rounds + 1
+        unit_grouped = {}
+        for rnd in range(first_up_round + TILES + 1):
+            up = rnd - first_up_round
+            now = [i for i in range(rnd * UNITS_PER_ROUND, (rnd + 1) * UNITS_PER_ROUND) if i < len(units)]
+            before = [i for i in range((rnd - 1) * UNITS_PER_ROUND, rnd * UNITS_PER_ROUND) if 0 <= i < len(units)]
+            if 0 <= up < TILES:
+                up_project(up)
+            unit_banks = {}
+            for i in now:
+                unit_banks[i] = transpose_unit(units[i])
+            if rnd < TILES:
+                add_residual(rnd)
+            if 1 <= rnd <= TILES:
+                normalise(rnd - 1)
+            if 2 <= rnd <= TILES + 1:
+                copy_out_m(rnd - 2)
+                quantise_m(rnd - 2)
+            if 1 <= up <= TILES:
+                gelu_and_store(up - 1, 0)
+            for i in now[:1]:
+                unit_grouped[i] = copy_out_unit(unit_banks[i])
+            if rnd < TILES:
+                inverse_rms(rnd)
+            if 1 <= up <= TILES:
+                gelu_and_store(up - 1, 1)
+            for i in now[1:]:
+                unit_grouped[i] = copy_out_unit(unit_banks[i])
+            if 0 <= up < TILES:
+                add_b1(up)
+            for i in before:
+                quantise_unit(units[i], unit_grouped[i])
+            if rnd + 1 < TILES:
+                project(rnd + 1)
+            if 1 <= rnd <= TILES:
+                transpose_m(rnd - 1)
+            if rnd == unit_rounds - 1:
+                for row in range(BO_ROWS + W2_ROWS, BO_ROWS + W2_ROWS + B1_ROWS):
+                    spread_row(row)
+            if 1 <= rnd <= POS:
+                add_bias_to_x(rnd + POS - 1)

@@ -112,16 +112,18 @@ def tile_transformerblock_pb_kernel(
         w2_all = spread[:, BO_ROWS : BO_ROWS + W2_ROWS, :].rearrange("p r n -> p (r n)")
         b1_all = spread[:, BO_ROWS + W2_ROWS :, :].rearrange("p r n -> p (r n)")
 
-        def spread_row(row):
-            bank = psum.tile([P, BANK], F32, tag="bank")
-            nc.tensor.matmul(
-                out=bank[:],
-                lhsT=ident_bf16[:, row : row + 1].to_broadcast([P, P]),
-                rhs=vector_rows[:],
-                start=True,
-                stop=True,
-            )
-            nc.scalar.copy(out=spread[:, row, :], in_=bank[:])
+        def spread_rows(first):
+            bank = psum.tile([P, 2, BANK], BF16, tag="bank")
+            for i in range(2):
+                row = first + i
+                nc.tensor.matmul(
+                    out=bank[:, i, :],
+                    lhsT=ident_bf16[:, row : row + 1].to_broadcast([P, P]),
+                    rhs=vector_rows[:],
+                    start=True,
+                    stop=True,
+                )
+            nc.scalar.copy(out=spread[:, first : first + 2, :], in_=bank[:])
 
         def token_unit(b, g):
             words = c_raw[b, g][:].bitcast(F32)
@@ -219,16 +221,15 @@ def tile_transformerblock_pb_kernel(
         m_tiles = {}
 
         def normalise(tile):
-            m_tiles[tile] = stream.tile([P, PACK, DIM // PACK], BF16, name="m_%d" % tile, tag="m")
-            x1_planes = x1_tiles[tile][:].rearrange("p (w t) -> p t w", t=PACK)
-            w2_planes = w2_all.rearrange("p (w t) -> p t w", t=PACK)
-            for e in range(2):
-                planes = slice(2 * e, 2 * e + 2)
+            m_tiles[tile] = stream.tile([P, HALVES, DIM // PACK, 2], BF16, name="m_%d" % tile, tag="m")
+            x1_halves = x1_tiles[tile][:].rearrange("p (q u e) -> p u q e", u=HALVES, e=2)
+            w2_halves = w2_all.rearrange("p (q u e) -> p u q e", u=HALVES, e=2)
+            for u in range(HALVES):
                 nc.vector.scalar_tensor_tensor(
-                    out=m_tiles[tile][:, planes, :],
-                    in0=x1_planes[:, planes, :],
+                    out=m_tiles[tile][:, u, :, :],
+                    in0=x1_halves[:, u, :, :],
                     scalar=inv_rms[:, tile : tile + 1],
-                    in1=w2_planes[:, planes, :],
+                    in1=w2_halves[:, u, :, :],
                     op0=ALU.mult,
                     op1=ALU.mult,
                 )
@@ -236,12 +237,12 @@ def tile_transformerblock_pb_kernel(
         m_banks = {}
 
         def transpose_m(tile):
-            m_banks[tile] = psum.tile([P, PASSES, PACK, P], BF16, tag="bank", name="m_bank_%d" % tile)
+            m_banks[tile] = psum.tile([P, PASSES, HALVES, P], F32, tag="bank", name="m_bank_%d" % tile)
+            words = m_tiles[tile][:].rearrange("p u q e -> p (u q e)").bitcast(F32)
             for g in range(PASSES):
-                for t in range(PACK):
-                    nc.tensor.transpose(
-                        m_banks[tile][:, g, t, :], m_tiles[tile][:, t, g * P : (g + 1) * P], ident_bf16[:]
-                    )
+                for u in range(HALVES):
+                    first = (u * PASSES + g) * P
+                    nc.tensor.transpose(m_banks[tile][:, g, u, :], words[:, first : first + P], ident_f32[:])
 
         grouped_m = {}
 
@@ -250,8 +251,8 @@ def tile_transformerblock_pb_kernel(
                 [P, PASSES * P * PACK], BF16, align_bytes=64, name="grouped_m_%d" % tile, tag="grouped_m"
             )
             nc.scalar.copy(
-                out=grouped_m[tile][:].rearrange("p (g r v) -> p g r v", g=PASSES, v=PACK),
-                in_=m_banks[tile][:].rearrange("p g v r -> p g r v"),
+                out=grouped_m[tile][:].bitcast(F32).rearrange("p (g r u) -> p g r u", g=PASSES, u=HALVES),
+                in_=m_banks[tile][:].rearrange("p g u r -> p g r u"),
             )
 
         def quantise_m(tile):
@@ -298,8 +299,8 @@ def tile_transformerblock_pb_kernel(
 
         token_units = [token_unit(0, g) for g in range(PASSES)]
         token_grouped = [copy_out_unit(transpose_unit(unit)) for unit in token_units]
-        for row in range(BO_ROWS + W2_ROWS):
-            spread_row(row)
+        for first in (0, BO_ROWS):
+            spread_rows(first)
         for unit, grouped in zip(token_units, token_grouped):
             quantise_unit(unit, grouped)
         wo_units = [weight_unit(wo_raw, wo_words, wo_scales, chunk, g) for chunk in range(2) for g in range(PASSES)]
@@ -310,7 +311,6 @@ def tile_transformerblock_pb_kernel(
             if i > 0:
                 quantise_unit(wo_units[i - 1], wo_grouped[i - 1])
         quantise_unit(wo_units[-1], wo_grouped[-1])
-        project(0)
 
         units = [weight_unit(w1_raw, w1_words, w1_scales, 0, g) for g in range(PASSES)]
         units += [token_unit(1, g) for g in range(PASSES)]
@@ -327,6 +327,8 @@ def tile_transformerblock_pb_kernel(
             unit_banks = {}
             for i in now:
                 unit_banks[i] = transpose_unit(units[i])
+                if i == 0:
+                    project(0)
             if rnd < TILES:
                 add_residual(rnd)
             if 1 <= rnd <= TILES:
@@ -353,7 +355,7 @@ def tile_transformerblock_pb_kernel(
             if 1 <= rnd <= TILES:
                 transpose_m(rnd - 1)
             if rnd == unit_rounds - 1:
-                for row in range(BO_ROWS + W2_ROWS, BO_ROWS + W2_ROWS + B1_ROWS):
-                    spread_row(row)
+                for first in range(BO_ROWS + W2_ROWS, BO_ROWS + W2_ROWS + B1_ROWS, 2):
+                    spread_rows(first)
             if 1 <= rnd <= POS:
                 add_bias_to_x(rnd + POS - 1)

@@ -80,8 +80,8 @@ def tile_transformerblock_pb_kernel(
         def load_weight(store, name, weight, chunk):
             store[chunk] = raw.tile([P, PACK * DIM], BF16, name="%s_%d" % (name, chunk))
             nc.sync.dma_start(
-                out=store[chunk][:].rearrange("p (a k) -> p a k", a=PACK),
-                in_=weight[chunk * BANK : (chunk + 1) * BANK, :].rearrange("(a p) k -> p a k", p=P),
+                out=store[chunk][:],
+                in_=weight[chunk * BANK : (chunk + 1) * BANK, :].rearrange("(p a) k -> p (a k)", a=PACK),
             )
 
         load_heads(0)
@@ -131,6 +131,7 @@ def tile_transformerblock_pb_kernel(
                 [words[:, j * PAIRS : (j + 1) * PAIRS] for j in range(POS)],
                 c_words[:, b, g, :, :].rearrange("p j r -> p (j r)"),
                 c_scales[:, b, g, :, :].rearrange("p j r -> p (j r)"),
+                True,
             )
 
         def weight_unit(w_raw, w_words, w_scales, chunk, g):
@@ -140,6 +141,7 @@ def tile_transformerblock_pb_kernel(
                 [words[:, (a * PASSES + g) * PAIRS : (a * PASSES + g + 1) * PAIRS] for a in range(PACK)],
                 w_words[:, g, cols],
                 w_scales[:, g, cols],
+                False,
             )
 
         def transpose_unit(unit):
@@ -155,14 +157,16 @@ def tile_transformerblock_pb_kernel(
                 banks.append(bank)
             return banks
 
-        def copy_out_unit(banks):
+        def copy_out_unit(banks, rows_are_tokens):
             grouped = stream.tile([P, PACK * BANK], BF16, align_bytes=64, bufs=2 * UNITS_PER_ROUND)
-            grouped_words = grouped[:].bitcast(F32).rearrange("p (i r u) -> p i r u", i=PACK, u=HALVES)
             for half in range(2):
-                nc.scalar.copy(
-                    out=grouped_words[:, 2 * half : 2 * half + 2, :, :],
-                    in_=banks[half][:].rearrange("p i u r -> p i r u"),
-                )
+                blocks = slice(2 * half, 2 * half + 2)
+                if rows_are_tokens:
+                    words = grouped[:].bitcast(F32).rearrange("p (i r u) -> p i r u", i=PACK, u=HALVES)
+                    nc.scalar.copy(out=words[:, blocks, :, :], in_=banks[half][:].rearrange("p i u r -> p i r u"))
+                else:
+                    words = grouped[:].bitcast(F32).rearrange("p (r i u) -> p r i u", i=PACK, u=HALVES)
+                    nc.scalar.copy(out=words[:, :, blocks, :], in_=banks[half][:].rearrange("p i u r -> p r i u"))
             return grouped
 
         def quantise_unit(unit, grouped):
@@ -298,7 +302,7 @@ def tile_transformerblock_pb_kernel(
             nc.sync.dma_start(out=out1_view[:, j, b, cols], in_=g_tiles[tile][:, cols])
 
         token_units = [token_unit(0, g) for g in range(PASSES)]
-        token_grouped = [copy_out_unit(transpose_unit(unit)) for unit in token_units]
+        token_grouped = [copy_out_unit(transpose_unit(unit), unit[3]) for unit in token_units]
         for first in (0, BO_ROWS):
             spread_rows(first)
         for unit, grouped in zip(token_units, token_grouped):
@@ -306,7 +310,7 @@ def tile_transformerblock_pb_kernel(
         wo_units = [weight_unit(wo_raw, wo_words, wo_scales, chunk, g) for chunk in range(2) for g in range(PASSES)]
         wo_grouped = []
         for i in range(len(wo_units)):
-            wo_grouped.append(copy_out_unit(transpose_unit(wo_units[i])))
+            wo_grouped.append(copy_out_unit(transpose_unit(wo_units[i]), wo_units[i][3]))
             add_bias_to_x(i)
             if i > 0:
                 quantise_unit(wo_units[i - 1], wo_grouped[i - 1])
@@ -339,13 +343,13 @@ def tile_transformerblock_pb_kernel(
             if 1 <= up <= TILES:
                 gelu_and_store(up - 1, 0)
             for i in now[:1]:
-                unit_grouped[i] = copy_out_unit(unit_banks[i])
+                unit_grouped[i] = copy_out_unit(unit_banks[i], units[i][3])
             if rnd < TILES:
                 inverse_rms(rnd)
             if 1 <= up <= TILES:
                 gelu_and_store(up - 1, 1)
             for i in now[1:]:
-                unit_grouped[i] = copy_out_unit(unit_banks[i])
+                unit_grouped[i] = copy_out_unit(unit_banks[i], units[i][3])
             if 0 <= up < TILES:
                 add_b1(up)
             for i in before:

@@ -53,7 +53,7 @@ def tile_transformerblock_pb_kernel(
         make_identity(nc, ident_bf16[:])
         nc.scalar.activation(out=table_warmer[:], in_=table_warmer[:], func=ACT.Gelu)
 
-        x_view = x.rearrange("(p j) b d -> p j b d", j=POS)
+        x_view = x.rearrange("(p j) b d -> p j (b d)", j=POS)
         out0_view = out_0.rearrange("(p j) b d -> p j b d", j=POS)
         out1_view = out_1.rearrange("(p j) b f -> p j b f", j=POS)
         c_raw = {}
@@ -68,9 +68,9 @@ def tile_transformerblock_pb_kernel(
                     out=c_raw[b, head][:], in_=h_attn[b, head].rearrange("(p j) d -> p (j d)", j=POS)
                 )
 
-        def load_x(b):
-            x_raw[b] = raw.tile([P, POS * DIM], BF16, name="x_raw_%d" % b)
-            nc.sync.dma_start(out=x_raw[b][:].rearrange("p (j d) -> p j d", j=POS), in_=x_view[:, :, b, :])
+        def load_x(j):
+            x_raw[j] = raw.tile([P, BATCH * DIM], BF16, name="x_raw_%d" % j)
+            nc.sync.dma_start(out=x_raw[j][:], in_=x_view[:, j, :])
 
         def load_vector(first_row, n_rows, vector):
             nc.sync.dma_start(
@@ -91,9 +91,11 @@ def tile_transformerblock_pb_kernel(
         load_x(0)
         load_weight(wo_raw, "wo_raw", out_proj_w, 0)
         load_weight(wo_raw, "wo_raw", out_proj_w, 1)
-        load_weight(w1_raw, "w1_raw", W1, 0)
-        load_heads(1)
         load_x(1)
+        load_weight(w1_raw, "w1_raw", W1, 0)
+        load_x(2)
+        load_heads(1)
+        load_x(3)
         load_weight(w1_raw, "w1_raw", W1, 1)
         load_weight(w1_raw, "w1_raw", W1, 2)
         load_weight(w1_raw, "w1_raw", W1, 3)
@@ -178,8 +180,24 @@ def tile_transformerblock_pb_kernel(
             b, j = divmod(tile, POS)
             x1_tiles[tile] = keep.tile([P, DIM], F32, name="x1_%d" % tile)
             nc.vector.tensor_tensor(
-                out=x1_tiles[tile][:], in0=x_raw[b][:, j * DIM : (j + 1) * DIM], in1=bo_all, op=ALU.add
+                out=x1_tiles[tile][:], in0=x_raw[j][:, b * DIM : (b + 1) * DIM], in1=bo_all, op=ALU.add
             )
+
+        def add_bias_to_x_in_psum(tile):
+            b, j = divmod(tile, POS)
+            x1_tiles[tile] = keep.tile([P, DIM], F32, name="x1_%d" % tile)
+            for n in range(DIM // BANK):
+                bank = psum.tile([P, BANK], F32, tag="bank")
+                cols = slice(b * DIM + n * BANK, b * DIM + (n + 1) * BANK)
+                nc.tensor.matmul(out=bank[:], lhsT=ident_bf16[:], rhs=x_raw[j][:, cols], start=True, stop=False)
+                nc.tensor.matmul(
+                    out=bank[:],
+                    lhsT=ident_bf16[:, n : n + 1].to_broadcast([P, P]),
+                    rhs=vector_rows[:],
+                    start=False,
+                    stop=True,
+                )
+                nc.scalar.copy(out=x1_tiles[tile][:, n * BANK : (n + 1) * BANK], in_=bank[:])
 
         attn_banks = {}
 
@@ -303,7 +321,7 @@ def tile_transformerblock_pb_kernel(
 
         token_units = [token_unit(0, g) for g in range(PASSES)]
         token_grouped = [copy_out_unit(transpose_unit(unit), unit[3]) for unit in token_units]
-        for first in (0, BO_ROWS):
+        for first in range(0, BO_ROWS + W2_ROWS + B1_ROWS, 2):
             spread_rows(first)
         for unit, grouped in zip(token_units, token_grouped):
             quantise_unit(unit, grouped)
@@ -311,7 +329,7 @@ def tile_transformerblock_pb_kernel(
         wo_grouped = []
         for i in range(len(wo_units)):
             wo_grouped.append(copy_out_unit(transpose_unit(wo_units[i]), wo_units[i][3]))
-            add_bias_to_x(i)
+            add_bias_to_x((0, 4, 1, 5)[i])
             if i > 0:
                 quantise_unit(wo_units[i - 1], wo_grouped[i - 1])
         quantise_unit(wo_units[-1], wo_grouped[-1])
@@ -356,10 +374,9 @@ def tile_transformerblock_pb_kernel(
                 quantise_unit(units[i], unit_grouped[i])
             if rnd + 1 < TILES:
                 project(rnd + 1)
+            if rnd == 5:
+                add_bias_to_x_in_psum(7)
             if 1 <= rnd <= TILES:
                 transpose_m(rnd - 1)
-            if rnd == unit_rounds - 1:
-                for first in range(BO_ROWS + W2_ROWS, BO_ROWS + W2_ROWS + B1_ROWS, 2):
-                    spread_rows(first)
-            if 1 <= rnd <= POS:
-                add_bias_to_x(rnd + POS - 1)
+            if rnd < 3:
+                add_bias_to_x((2, 3, 6,)[rnd])

@@ -243,7 +243,7 @@ def tile_transformerblock_pb_kernel(
         m_tiles = {}
 
         def normalise(tile):
-            m_tiles[tile] = stream.tile([P, HALVES, DIM // PACK, 2], BF16, name="m_%d" % tile, tag="m")
+            m_tiles[tile] = stream.tile([P, HALVES, DIM // PACK, 2], BF16, name="m_%d" % tile, tag="m", bufs=2)
             x1_halves = x1_tiles[tile][:].rearrange("p (q u e) -> p u q e", u=HALVES, e=2)
             w2_halves = w2_all.rearrange("p (q u e) -> p u q e", u=HALVES, e=2)
             for u in range(HALVES):
@@ -270,7 +270,7 @@ def tile_transformerblock_pb_kernel(
 
         def copy_out_m(tile):
             grouped_m[tile] = stream.tile(
-                [P, PASSES * P * PACK], BF16, align_bytes=64, name="grouped_m_%d" % tile, tag="grouped_m"
+                [P, PASSES * P * PACK], BF16, align_bytes=64, name="grouped_m_%d" % tile, tag="grouped_m", bufs=2
             )
             nc.scalar.copy(
                 out=grouped_m[tile][:].bitcast(F32).rearrange("p (g r u) -> p g r u", g=PASSES, u=HALVES),
@@ -304,7 +304,7 @@ def tile_transformerblock_pb_kernel(
         g_tiles = {}
 
         def add_b1(tile):
-            g_tiles[tile] = stream.tile([P, FF], F32, name="g_%d" % tile, tag="g")
+            g_tiles[tile] = stream.tile([P, FF], F32, name="g_%d" % tile, tag="g", bufs=4)
             for n in range(FF // BANK):
                 cols = slice(n * BANK, (n + 1) * BANK)
                 nc.vector.tensor_tensor(
@@ -321,62 +321,76 @@ def tile_transformerblock_pb_kernel(
 
         token_units = [token_unit(0, g) for g in range(PASSES)]
         token_grouped = [copy_out_unit(transpose_unit(unit), unit[3]) for unit in token_units]
-        for first in range(0, BO_ROWS + W2_ROWS + B1_ROWS, 2):
-            spread_rows(first)
+        spread_rows(0)
+        spread_rows(2)
+        spread_rows(4)
+        spread_rows(6)
         for unit, grouped in zip(token_units, token_grouped):
             quantise_unit(unit, grouped)
         wo_units = [weight_unit(wo_raw, wo_words, wo_scales, chunk, g) for chunk in range(2) for g in range(PASSES)]
         wo_grouped = []
-        for i in range(len(wo_units)):
-            wo_grouped.append(copy_out_unit(transpose_unit(wo_units[i]), wo_units[i][3]))
-            add_bias_to_x((0, 4, 1, 5)[i])
-            if i > 0:
-                quantise_unit(wo_units[i - 1], wo_grouped[i - 1])
-        quantise_unit(wo_units[-1], wo_grouped[-1])
+        wo_grouped.append(copy_out_unit(transpose_unit(wo_units[0]), wo_units[0][3]))
+        add_bias_to_x(0)
+        wo_grouped.append(copy_out_unit(transpose_unit(wo_units[1]), wo_units[1][3]))
+        add_bias_to_x(4)
+        quantise_unit(wo_units[0], wo_grouped[0])
+        wo_grouped.append(copy_out_unit(transpose_unit(wo_units[2]), wo_units[2][3]))
+        add_bias_to_x(1)
+        quantise_unit(wo_units[1], wo_grouped[1])
+        wo_grouped.append(copy_out_unit(transpose_unit(wo_units[3]), wo_units[3][3]))
+        add_bias_to_x(5)
+        quantise_unit(wo_units[2], wo_grouped[2])
+        quantise_unit(wo_units[3], wo_grouped[3])
 
         units = [weight_unit(w1_raw, w1_words, w1_scales, 0, g) for g in range(PASSES)]
         units += [token_unit(1, g) for g in range(PASSES)]
         units += [weight_unit(w1_raw, w1_words, w1_scales, chunk, g) for chunk in (1, 2, 3) for g in range(PASSES)]
-        unit_rounds = (len(units) + UNITS_PER_ROUND - 1) // UNITS_PER_ROUND
-        first_up_round = unit_rounds + 1
+        first_unit = (0, 2, 4, 6, 8, 10)
+        unit_rounds = 5
+        first_up_round = 6
         unit_grouped = {}
         for rnd in range(first_up_round + TILES + 1):
             up = rnd - first_up_round
-            now = [i for i in range(rnd * UNITS_PER_ROUND, (rnd + 1) * UNITS_PER_ROUND) if i < len(units)]
-            before = [i for i in range((rnd - 1) * UNITS_PER_ROUND, rnd * UNITS_PER_ROUND) if 0 <= i < len(units)]
-            if 0 <= up < TILES:
-                up_project(up)
+            now = list(range(first_unit[rnd], first_unit[rnd + 1])) if rnd < unit_rounds else []
+            before = list(range(first_unit[rnd - 1], first_unit[rnd])) if 1 <= rnd <= unit_rounds else []
             unit_banks = {}
+            m_tile = rnd - 2
             for i in now:
                 unit_banks[i] = transpose_unit(units[i])
                 if i == 0:
                     project(0)
+                    project(1)
+                if i == now[0] and 0 <= m_tile < TILES:
+                    transpose_m(m_tile)
+            if not now and 0 <= m_tile < TILES and 1:
+                transpose_m(m_tile)
+            if 0 <= up < TILES:
+                up_project(up)
             if rnd < TILES:
                 add_residual(rnd)
-            if 1 <= rnd <= TILES:
-                normalise(rnd - 1)
-            if 2 <= rnd <= TILES + 1:
-                copy_out_m(rnd - 2)
-                quantise_m(rnd - 2)
-            if 1 <= up <= TILES:
-                gelu_and_store(up - 1, 0)
-            for i in now[:1]:
-                unit_grouped[i] = copy_out_unit(unit_banks[i], units[i][3])
-            if rnd < TILES:
-                inverse_rms(rnd)
-            if 1 <= up <= TILES:
-                gelu_and_store(up - 1, 1)
-            for i in now[1:]:
-                unit_grouped[i] = copy_out_unit(unit_banks[i], units[i][3])
-            if 0 <= up < TILES:
-                add_b1(up)
             for i in before:
                 quantise_unit(units[i], unit_grouped[i])
-            if rnd + 1 < TILES:
-                project(rnd + 1)
-            if rnd == 5:
-                add_bias_to_x_in_psum(7)
             if 1 <= rnd <= TILES:
-                transpose_m(rnd - 1)
-            if rnd < 3:
-                add_bias_to_x((2, 3, 6,)[rnd])
+                normalise(rnd - 1)
+            for i in now[:1]:
+                unit_grouped[i] = copy_out_unit(unit_banks[i], units[i][3])
+            if not now and 0 <= m_tile < TILES and not 1:
+                transpose_m(m_tile)
+            if 0 <= m_tile < TILES:
+                copy_out_m(m_tile)
+            if rnd < TILES:
+                inverse_rms(rnd)
+            for i in now[1:]:
+                unit_grouped[i] = copy_out_unit(unit_banks[i], units[i][3])
+            if 0 <= m_tile - 1 < TILES:
+                quantise_m(m_tile - 1)
+            if 0 <= up < TILES:
+                add_b1(up)
+                gelu_and_store(up, 0)
+                gelu_and_store(up, 1)
+            if 1 < rnd + 1 < TILES:
+                project(rnd + 1)
+            for tile in {5: (7,)}.get(rnd, ()):
+                add_bias_to_x_in_psum(tile)
+            for tile in {0: (2,), 1: (3,), 2: (6,)}.get(rnd, ()):
+                add_bias_to_x(tile)

@@ -100,14 +100,14 @@ def tile_transformerblock_pb_kernel(
         load_weight(w1_raw, "w1_raw", W1, 2)
         load_weight(w1_raw, "w1_raw", W1, 3)
 
-        c_words = keep.tile([P, BATCH, PASSES, POS, P], U32, align_bytes=64)
-        c_scales = keep.tile([P, BATCH, PASSES, POS, P], U8, align_bytes=64)
-        m_words = keep.tile([P, TILES, PASSES, P], U32, align_bytes=64)
-        m_scales = keep.tile([P, TILES, PASSES, P], U8, align_bytes=64)
-        wo_words = keep.tile([P, PASSES, DIM], U32, align_bytes=64)
-        wo_scales = keep.tile([P, PASSES, DIM], U8, align_bytes=64)
-        w1_words = keep.tile([P, PASSES, FF], U32, align_bytes=64)
-        w1_scales = keep.tile([P, PASSES, FF], U8, align_bytes=64)
+        c_words = keep.tile([P, BATCH, PASSES, POS, P], U32, align_bytes=256)
+        c_scales = keep.tile([P, BATCH, PASSES, POS, P], U8, align_bytes=256)
+        m_words = keep.tile([P, TILES, PASSES, P], U32, align_bytes=256)
+        m_scales = keep.tile([P, TILES, PASSES, P], U8, align_bytes=256)
+        wo_words = keep.tile([P, PASSES, DIM], U32, align_bytes=256)
+        wo_scales = keep.tile([P, PASSES, DIM], U8, align_bytes=256)
+        w1_words = keep.tile([P, PASSES, FF], U32, align_bytes=256)
+        w1_scales = keep.tile([P, PASSES, FF], U8, align_bytes=256)
 
         spread = const.tile([P, BO_ROWS + W2_ROWS + B1_ROWS, BANK], BF16)
         bo_all = spread[:, 0:BO_ROWS, :].rearrange("p r n -> p (r n)")

@@ -88,8 +88,8 @@ def tile_transformerblock_pb_kernel(
         load_vector(0, BO_ROWS, out_proj_b)
         load_vector(BO_ROWS, W2_ROWS, w_norm2)
         load_vector(BO_ROWS + W2_ROWS, B1_ROWS, b1)
-        load_x(0)
         load_weight(wo_raw, "wo_raw", out_proj_w, 0)
+        load_x(0)
         load_weight(wo_raw, "wo_raw", out_proj_w, 1)
         load_x(1)
         load_weight(w1_raw, "w1_raw", W1, 0)
@@ -323,8 +323,6 @@ def tile_transformerblock_pb_kernel(
         token_grouped = [copy_out_unit(transpose_unit(unit), unit[3]) for unit in token_units]
         spread_rows(0)
         spread_rows(2)
-        spread_rows(4)
-        spread_rows(6)
         for unit, grouped in zip(token_units, token_grouped):
             quantise_unit(unit, grouped)
         wo_units = [weight_unit(wo_raw, wo_words, wo_scales, chunk, g) for chunk in range(2) for g in range(PASSES)]
@@ -333,11 +331,13 @@ def tile_transformerblock_pb_kernel(
         add_bias_to_x(0)
         wo_grouped.append(copy_out_unit(transpose_unit(wo_units[1]), wo_units[1][3]))
         add_bias_to_x(4)
+        spread_rows(4)
         quantise_unit(wo_units[0], wo_grouped[0])
         wo_grouped.append(copy_out_unit(transpose_unit(wo_units[2]), wo_units[2][3]))
         add_bias_to_x(1)
         quantise_unit(wo_units[1], wo_grouped[1])
         wo_grouped.append(copy_out_unit(transpose_unit(wo_units[3]), wo_units[3][3]))
+        spread_rows(6)
         add_bias_to_x(5)
         quantise_unit(wo_units[2], wo_grouped[2])
         quantise_unit(wo_units[3], wo_grouped[3])

@@ -24,6 +24,8 @@ PAIRS = K_PASS // 2
 HALVES = PAIRS // P
 EPS = 1e-8
 BO_ROWS, W2_ROWS, B1_ROWS = DIM // BANK, DIM // BANK, FF // BANK
+G_BUFS = 8
+LAG_A, LAG_B = 4, 6
 UNITS_PER_ROUND = 2
 
 FLOPS = 2 * SEQ * BATCH * DIM * (DIM + FF)
@@ -286,8 +288,8 @@ def tile_transformerblock_pb_kernel(
 
         up_banks = {}
 
-        def up_project(tile):
-            for n in range(FF // BANK):
+        def up_project(tile, half):
+            for n in (2 * half, 2 * half + 1):
                 cols = slice(n * BANK, (n + 1) * BANK)
                 up_banks[tile, n] = psum.tile([P, BANK], F32, tag="bank", name="up_%d_%d" % (tile, n))
                 for g in range(PASSES):
@@ -303,21 +305,25 @@ def tile_transformerblock_pb_kernel(
 
         g_tiles = {}
 
-        def add_b1(tile):
-            g_tiles[tile] = stream.tile([P, FF], F32, name="g_%d" % tile, tag="g", bufs=4)
-            for n in range(FF // BANK):
-                cols = slice(n * BANK, (n + 1) * BANK)
+        def add_b1(tile, half):
+            g_tiles[tile, half] = stream.tile([P, FF // 2], F32, name="g_%d_%d" % (tile, half), tag="g", bufs=G_BUFS)
+            for i in range(2):
+                n = 2 * half + i
                 nc.vector.tensor_tensor(
-                    out=g_tiles[tile][:, cols], in0=up_banks[tile, n][:], in1=b1_all[:, cols], op=ALU.add
+                    out=g_tiles[tile, half][:, i * BANK : (i + 1) * BANK],
+                    in0=up_banks[tile, n][:],
+                    in1=b1_all[:, n * BANK : (n + 1) * BANK],
+                    op=ALU.add,
                 )
 
         def gelu_and_store(tile, half):
             b, j = divmod(tile, POS)
-            for n in (2 * half, 2 * half + 1):
-                cols = slice(n * BANK, (n + 1) * BANK)
-                nc.scalar.activation(out=g_tiles[tile][:, cols], in_=g_tiles[tile][:, cols], func=ACT.Gelu)
-            cols = slice(half * FF // 2, (half + 1) * FF // 2)
-            nc.sync.dma_start(out=out1_view[:, j, b, cols], in_=g_tiles[tile][:, cols])
+            for i in range(2):
+                cols = slice(i * BANK, (i + 1) * BANK)
+                nc.scalar.activation(out=g_tiles[tile, half][:, cols], in_=g_tiles[tile, half][:, cols], func=ACT.Gelu)
+            nc.sync.dma_start(
+                out=out1_view[:, j, b, half * FF // 2 : (half + 1) * FF // 2], in_=g_tiles[tile, half][:]
+            )
 
         token_units = [token_unit(0, g) for g in range(PASSES)]
         token_grouped = [copy_out_unit(transpose_unit(unit), unit[3]) for unit in token_units]
@@ -347,10 +353,8 @@ def tile_transformerblock_pb_kernel(
         units += [weight_unit(w1_raw, w1_words, w1_scales, chunk, g) for chunk in (1, 2, 3) for g in range(PASSES)]
         first_unit = (0, 2, 4, 6, 8, 10)
         unit_rounds = 5
-        first_up_round = 6
         unit_grouped = {}
-        for rnd in range(first_up_round + TILES + 1):
-            up = rnd - first_up_round
+        for rnd in range(LAG_B + TILES):
             now = list(range(first_unit[rnd], first_unit[rnd + 1])) if rnd < unit_rounds else []
             before = list(range(first_unit[rnd - 1], first_unit[rnd])) if 1 <= rnd <= unit_rounds else []
             unit_banks = {}
@@ -364,8 +368,9 @@ def tile_transformerblock_pb_kernel(
                     transpose_m(m_tile)
             if not now and 0 <= m_tile < TILES and 1:
                 transpose_m(m_tile)
-            if 0 <= up < TILES:
-                up_project(up)
+            ups = [(rnd - lag, half) for half, lag in ((1, LAG_B), (0, LAG_A)) if 0 <= rnd - lag < TILES]
+            for tile, half in ups:
+                up_project(tile, half)
             if rnd < TILES:
                 add_residual(rnd)
             for i in before:
@@ -384,10 +389,9 @@ def tile_transformerblock_pb_kernel(
                 unit_grouped[i] = copy_out_unit(unit_banks[i], units[i][3])
             if 0 <= m_tile - 1 < TILES:
                 quantise_m(m_tile - 1)
-            if 0 <= up < TILES:
-                add_b1(up)
-                gelu_and_store(up, 0)
-                gelu_and_store(up, 1)
+            for tile, half in ups:
+                add_b1(tile, half)
+                gelu_and_store(tile, half)
             if 1 < rnd + 1 < TILES:
                 project(rnd + 1)
             for tile in {5: (7,)}.get(rnd, ()):

@@ -25,7 +25,6 @@ HALVES = PAIRS // P
 EPS = 1e-8
 BO_ROWS, W2_ROWS, B1_ROWS = DIM // BANK, DIM // BANK, FF // BANK
 G_BUFS = 8
-LAG_A, LAG_B = 4, 6
 UNITS_PER_ROUND = 2
 
 FLOPS = 2 * SEQ * BATCH * DIM * (DIM + FF)
@@ -49,10 +48,10 @@ def tile_transformerblock_pb_kernel(
         nc.vector.memset(table_warmer[:], 0.0)
         minus_half = const.tile([P, 1], F32)
         nc.vector.memset(minus_half[:], -0.5)
-        ident_f32 = const.tile([P, P], F32)
-        make_identity(nc, ident_f32[:])
         ident_bf16 = const.tile([P, P], BF16)
         make_identity(nc, ident_bf16[:])
+        ident_f32 = const.tile([P, P], F32)
+        make_identity(nc, ident_f32[:])
         nc.scalar.activation(out=table_warmer[:], in_=table_warmer[:], func=ACT.Gelu)
 
         x_view = x.rearrange("(p j) b d -> p j (b d)", j=POS)
@@ -63,8 +62,8 @@ def tile_transformerblock_pb_kernel(
         wo_raw = {}
         w1_raw = {}
 
-        def load_heads(b):
-            for head in range(HEADS):
+        def load_heads(b, heads=range(HEADS)):
+            for head in heads:
                 c_raw[b, head] = raw.tile([P, POS * HEAD_DIM], BF16, name="c_raw_%d_%d" % (b, head))
                 nc.sync.dma_start(
                     out=c_raw[b, head][:], in_=h_attn[b, head].rearrange("(p j) d -> p (j d)", j=POS)
@@ -86,21 +85,20 @@ def tile_transformerblock_pb_kernel(
                 in_=weight[chunk * BANK : (chunk + 1) * BANK, :].rearrange("(p a) k -> p (a k)", a=PACK),
             )
 
-        load_heads(0)
         load_vector(0, BO_ROWS, out_proj_b)
         load_vector(BO_ROWS, W2_ROWS, w_norm2)
         load_vector(BO_ROWS + W2_ROWS, B1_ROWS, b1)
-        load_weight(wo_raw, "wo_raw", out_proj_w, 0)
+        load_heads(0, (0,))
         load_x(0)
+        load_heads(0, (1,))
+        load_weight(wo_raw, "wo_raw", out_proj_w, 0)
         load_weight(wo_raw, "wo_raw", out_proj_w, 1)
         load_x(1)
-        load_weight(w1_raw, "w1_raw", W1, 0)
-        load_x(2)
         load_heads(1)
+        load_x(2)
         load_x(3)
-        load_weight(w1_raw, "w1_raw", W1, 1)
-        load_weight(w1_raw, "w1_raw", W1, 2)
-        load_weight(w1_raw, "w1_raw", W1, 3)
+        for chunk in range(FF // BANK):
+            load_weight(w1_raw, "w1_raw", W1, chunk)
 
         c_words = keep.tile([P, BATCH, PASSES, POS, P], U32, align_bytes=256)
         c_scales = keep.tile([P, BATCH, PASSES, POS, P], U8, align_bytes=256)
@@ -116,8 +114,11 @@ def tile_transformerblock_pb_kernel(
         w2_all = spread[:, BO_ROWS : BO_ROWS + W2_ROWS, :].rearrange("p r n -> p (r n)")
         b1_all = spread[:, BO_ROWS + W2_ROWS :, :].rearrange("p r n -> p (r n)")
 
-        def spread_rows(first):
-            bank = psum.tile([P, 2, BANK], BF16, tag="bank")
+        spread_banks = {}
+
+        def spread_matmuls(first):
+            bank = psum.tile([P, 2, BANK], BF16, tag="bank", name="spread_%d" % first)
+            spread_banks[first] = bank
             for i in range(2):
                 row = first + i
                 nc.tensor.matmul(
@@ -127,7 +128,9 @@ def tile_transformerblock_pb_kernel(
                     start=True,
                     stop=True,
                 )
-            nc.scalar.copy(out=spread[:, first : first + 2, :], in_=bank[:])
+
+        def copy_out_spread(first, copy):
+            copy(out=spread[:, first : first + 2, :], in_=spread_banks[first][:])
 
         def token_unit(b, g):
             words = c_raw[b, g][:].bitcast(F32)
@@ -148,30 +151,24 @@ def tile_transformerblock_pb_kernel(
                 False,
             )
 
-        def transpose_unit(unit):
-            blocks = unit[0]
-            banks = []
-            for half in range(2):
-                bank = psum.tile([P, 2, HALVES, P], F32, tag="bank")
-                for i in range(2):
-                    for u in range(HALVES):
-                        nc.tensor.transpose(
-                            bank[:, i, u, :], blocks[2 * half + i][:, u::HALVES], ident_f32[:]
-                        )
-                banks.append(bank)
-            return banks
+        def transpose_half(unit, half, i):
+            bank = psum.tile([P, 2, HALVES, P], F32, tag="bank", name="unit_%d_%d" % (i, half))
+            for k in range(2):
+                for u in range(HALVES):
+                    nc.tensor.transpose(bank[:, k, u, :], unit[0][2 * half + k][:, u::HALVES], ident_f32[:])
+            return bank
 
-        def copy_out_unit(banks, rows_are_tokens):
-            grouped = stream.tile([P, PACK * BANK], BF16, align_bytes=64, bufs=2 * UNITS_PER_ROUND)
-            for half in range(2):
-                blocks = slice(2 * half, 2 * half + 2)
-                if rows_are_tokens:
-                    words = grouped[:].bitcast(F32).rearrange("p (i r u) -> p i r u", i=PACK, u=HALVES)
-                    nc.scalar.copy(out=words[:, blocks, :, :], in_=banks[half][:].rearrange("p i u r -> p i r u"))
-                else:
-                    words = grouped[:].bitcast(F32).rearrange("p (r i u) -> p r i u", i=PACK, u=HALVES)
-                    nc.scalar.copy(out=words[:, :, blocks, :], in_=banks[half][:].rearrange("p i u r -> p r i u"))
-            return grouped
+        def new_grouped(i):
+            return stream.tile([P, PACK * BANK], BF16, align_bytes=64, name="grouped_%d" % i, tag="grouped", bufs=2 * UNITS_PER_ROUND)
+
+        def copy_out_half(banks, grouped, rows_are_tokens, half, copy):
+            blocks = slice(2 * half, 2 * half + 2)
+            if rows_are_tokens:
+                words = grouped[:].bitcast(F32).rearrange("p (i r u) -> p i r u", i=PACK, u=HALVES)
+                copy(out=words[:, blocks, :, :], in_=banks[half][:].rearrange("p i u r -> p i r u"))
+            else:
+                words = grouped[:].bitcast(F32).rearrange("p (r i u) -> p r i u", i=PACK, u=HALVES)
+                copy(out=words[:, :, blocks, :], in_=banks[half][:].rearrange("p i u r -> p r i u"))
 
         def quantise_unit(unit, grouped):
             nc.vector.quantize_mx(out=unit[1].bitcast(FP8X4), scales=unit[2], in_=grouped[:])
@@ -185,11 +182,26 @@ def tile_transformerblock_pb_kernel(
                 out=x1_tiles[tile][:], in0=x_raw[j][:, b * DIM : (b + 1) * DIM], in1=bo_all, op=ALU.add
             )
 
-        def add_bias_to_x_in_psum(tile):
+        def add_bias_to_x_on_gpsimd(tile):
             b, j = divmod(tile, POS)
             x1_tiles[tile] = keep.tile([P, DIM], F32, name="x1_%d" % tile)
             for n in range(DIM // BANK):
-                bank = psum.tile([P, BANK], F32, tag="bank")
+                cols = slice(n * BANK, (n + 1) * BANK)
+                nc.gpsimd.tensor_tensor(
+                    out=x1_tiles[tile][:, cols],
+                    in0=x_raw[j][:, b * DIM + n * BANK : b * DIM + (n + 1) * BANK],
+                    in1=bo_all[:, cols],
+                    op=ALU.add,
+                )
+
+        xb_banks = {}
+
+        def sum_bias_and_x(tile):
+            b, j = divmod(tile, POS)
+            x1_tiles[tile] = keep.tile([P, DIM], F32, name="x1_%d" % tile)
+            for n in range(DIM // BANK):
+                bank = psum.tile([P, BANK], F32, tag="bank", name="xb_%d_%d" % (tile, n))
+                xb_banks[tile, n] = bank
                 cols = slice(b * DIM + n * BANK, b * DIM + (n + 1) * BANK)
                 nc.tensor.matmul(out=bank[:], lhsT=ident_bf16[:], rhs=x_raw[j][:, cols], start=True, stop=False)
                 nc.tensor.matmul(
@@ -199,13 +211,16 @@ def tile_transformerblock_pb_kernel(
                     start=False,
                     stop=True,
                 )
-                nc.scalar.copy(out=x1_tiles[tile][:, n * BANK : (n + 1) * BANK], in_=bank[:])
+
+        def copy_out_bias_and_x(tile):
+            for n in range(DIM // BANK):
+                nc.scalar.copy(out=x1_tiles[tile][:, n * BANK : (n + 1) * BANK], in_=xb_banks[tile, n][:])
 
         attn_banks = {}
 
-        def project(tile):
+        def project(tile, halves=range(DIM // BANK)):
             b, j = divmod(tile, POS)
-            for n in range(DIM // BANK):
+            for n in halves:
                 cols = slice(n * BANK, (n + 1) * BANK)
                 attn_banks[tile, n] = psum.tile([P, BANK], F32, tag="bank", name="attn_%d_%d" % (tile, n))
                 for g in range(PASSES):
@@ -231,12 +246,15 @@ def tile_transformerblock_pb_kernel(
         mean_sq_eps = const.tile([P, TILES], F32)
         inv_rms = const.tile([P, TILES], F32)
 
-        def inverse_rms(tile):
+        def sum_squares(tile):
             col = slice(tile, tile + 1)
             squares = stream.tile([P, DIM], BF16, bufs=2)
             nc.scalar.activation(
                 out=squares[:], in_=x1_tiles[tile][:], func=ACT.Square, scale=DIM**-0.5, accum_out=mean_sq[:, col]
             )
+
+        def inverse_rms(tile):
+            col = slice(tile, tile + 1)
             nc.gpsimd.tensor_scalar(
                 out=mean_sq_eps[:, col], in0=mean_sq[:, col], scalar1=EPS, scalar2=1.0, op0=ALU.add, op1=ALU.mult
             )
@@ -256,6 +274,21 @@ def tile_transformerblock_pb_kernel(
                     in1=w2_halves[:, u, :, :],
                     op0=ALU.mult,
                     op1=ALU.mult,
+                )
+
+        n_tiles = {}
+
+        def scale_rows(tile):
+            n_tiles[tile] = stream.tile([P, DIM], F32, name="n_%d" % tile, tag="n", bufs=1)
+            nc.scalar.activation(out=n_tiles[tile][:], in_=x1_tiles[tile][:], func=ACT.Copy, scale=inv_rms[:, tile : tile + 1])
+
+        def weight_columns(tile):
+            m_tiles[tile] = stream.tile([P, HALVES, DIM // PACK, 2], BF16, name="m_%d" % tile, tag="m", bufs=2)
+            n_halves = n_tiles[tile][:].rearrange("p (q u e) -> p u q e", u=HALVES, e=2)
+            w2_halves = w2_all.rearrange("p (q u e) -> p u q e", u=HALVES, e=2)
+            for u in range(HALVES):
+                nc.gpsimd.tensor_tensor(
+                    out=m_tiles[tile][:, u, :, :], in0=n_halves[:, u, :, :], in1=w2_halves[:, u, :, :], op=ALU.mult
                 )
 
         m_banks = {}
@@ -325,76 +358,100 @@ def tile_transformerblock_pb_kernel(
                 out=out1_view[:, j, b, half * FF // 2 : (half + 1) * FF // 2], in_=g_tiles[tile, half][:]
             )
 
-        token_units = [token_unit(0, g) for g in range(PASSES)]
-        token_grouped = [copy_out_unit(transpose_unit(unit), unit[3]) for unit in token_units]
-        spread_rows(0)
-        spread_rows(2)
-        for unit, grouped in zip(token_units, token_grouped):
-            quantise_unit(unit, grouped)
-        wo_units = [weight_unit(wo_raw, wo_words, wo_scales, chunk, g) for chunk in range(2) for g in range(PASSES)]
-        wo_grouped = []
-        wo_grouped.append(copy_out_unit(transpose_unit(wo_units[0]), wo_units[0][3]))
-        add_bias_to_x(0)
-        wo_grouped.append(copy_out_unit(transpose_unit(wo_units[1]), wo_units[1][3]))
-        add_bias_to_x(4)
-        spread_rows(4)
-        quantise_unit(wo_units[0], wo_grouped[0])
-        wo_grouped.append(copy_out_unit(transpose_unit(wo_units[2]), wo_units[2][3]))
-        add_bias_to_x(1)
-        quantise_unit(wo_units[1], wo_grouped[1])
-        wo_grouped.append(copy_out_unit(transpose_unit(wo_units[3]), wo_units[3][3]))
-        spread_rows(6)
-        add_bias_to_x(5)
-        quantise_unit(wo_units[2], wo_grouped[2])
-        quantise_unit(wo_units[3], wo_grouped[3])
+        def transpose_unit(unit, i):
+            return [transpose_half(unit, half, i) for half in range(2)]
 
-        units = [weight_unit(w1_raw, w1_words, w1_scales, 0, g) for g in range(PASSES)]
-        units += [token_unit(1, g) for g in range(PASSES)]
-        units += [weight_unit(w1_raw, w1_words, w1_scales, chunk, g) for chunk in (1, 2, 3) for g in range(PASSES)]
-        first_unit = (0, 2, 4, 6, 8, 10)
+        def copy_out_unit(banks, grouped, rows_are_tokens, copies=(nc.scalar.copy, nc.scalar.copy)):
+            for half in range(2):
+                copy_out_half(banks, grouped, rows_are_tokens, half, copies[half])
+
+        for first in range(0, 8, 2):
+            spread_matmuls(first)
+        for first in range(0, 8, 2):
+            copy_out_spread(first, nc.vector.tensor_copy if first % 4 == 0 else nc.scalar.copy)
+        add_bias_to_x_on_gpsimd(0)
+        add_bias_to_x_on_gpsimd(4)
+        head_units = [token_unit(0, q) for q in range(PASSES)]
+        head_units += [weight_unit(wo_raw, wo_words, wo_scales, chunk, q) for chunk in range(2) for q in range(PASSES)]
+        head_grouped = {}
+        for i in range(2):
+            banks = transpose_unit(head_units[i], i)
+            head_grouped[i] = new_grouped(i)
+            copy_out_unit(banks, head_grouped[i], True, (nc.vector.tensor_copy, nc.scalar.copy))
+        quantise_unit(head_units[0], head_grouped[0])
+        quantise_unit(head_units[1], head_grouped[1])
+        for i in range(2, 6):
+            banks = transpose_unit(head_units[i], i)
+            head_grouped[i] = new_grouped(i)
+            copy_out_unit(banks, head_grouped[i], False)
+            if i == 3:
+                add_bias_to_x(5)
+            if i == 5:
+                add_bias_to_x(1)
+            quantise_unit(head_units[i], head_grouped[i])
+
+        units = [token_unit(1, q) for q in range(PASSES)]
+        units += [weight_unit(w1_raw, w1_words, w1_scales, chunk, q) for chunk in range(4) for q in range(PASSES)]
         unit_rounds = 5
-        unit_grouped = {}
-        for rnd in range(LAG_B + TILES):
-            now = list(range(first_unit[rnd], first_unit[rnd + 1])) if rnd < unit_rounds else []
-            before = list(range(first_unit[rnd - 1], first_unit[rnd])) if 1 <= rnd <= unit_rounds else []
-            unit_banks = {}
+        grouped = {}
+        for rnd in range(6 + TILES):
+            now = (2 * rnd, 2 * rnd + 1) if rnd < unit_rounds else ()
+            up = rnd - 6
             m_tile = rnd - 2
-            for i in now:
-                unit_banks[i] = transpose_unit(units[i])
-                if i == 0:
-                    project(0)
-                    project(1)
-                if i == now[0] and 0 <= m_tile < TILES:
-                    transpose_m(m_tile)
-            if not now and 0 <= m_tile < TILES and 1:
-                transpose_m(m_tile)
-            ups = [(rnd - lag, half) for half, lag in ((1, LAG_B), (0, LAG_A)) if 0 <= rnd - lag < TILES]
-            for tile, half in ups:
-                up_project(tile, half)
+            banks = {}
+            if 0 <= up < TILES:
+                up_project(up, 0)
+            if 1 < rnd + 1 < TILES:
+                project(rnd + 1, (0,))
+            if rnd == 5:
+                sum_bias_and_x(6)
+            if rnd == 0:
+                banks[0] = transpose_unit(units[0], 6)
+                project(0)
+                project(1)
             if rnd < TILES:
                 add_residual(rnd)
-            for i in before:
-                quantise_unit(units[i], unit_grouped[i])
-            if 1 <= rnd <= TILES:
-                normalise(rnd - 1)
-            for i in now[:1]:
-                unit_grouped[i] = copy_out_unit(unit_banks[i], units[i][3])
-            if not now and 0 <= m_tile < TILES and not 1:
-                transpose_m(m_tile)
-            if 0 <= m_tile < TILES:
-                copy_out_m(m_tile)
+            for tile in {1: (2, 7)}.get(rnd, ()):
+                add_bias_to_x(tile)
+            for tile in {0: (3,)}.get(rnd, ()):
+                add_bias_to_x_on_gpsimd(tile)
+            if 0 <= up < TILES:
+                add_b1(up, 0)
+                up_project(up, 1)
+            if now and rnd:
+                banks[now[0]] = transpose_unit(units[now[0]], now[0] + 6)
+            if now:
+                grouped[now[0]] = new_grouped(now[0] + 6)
+                copy_out_unit(banks[now[0]], grouped[now[0]], units[now[0]][3])
+            if rnd == 5:
+                copy_out_bias_and_x(6)
             if rnd < TILES:
+                sum_squares(rnd)
                 inverse_rms(rnd)
-            for i in now[1:]:
-                unit_grouped[i] = copy_out_unit(unit_banks[i], units[i][3])
+            if 1 < rnd + 1 < TILES:
+                project(rnd + 1, (1,))
+            if 0 <= m_tile < TILES:
+                transpose_m(m_tile)
+            if now:
+                banks[now[1]] = transpose_unit(units[now[1]], now[1] + 6)
+            if 1 <= rnd <= TILES:
+                if rnd - 1 == 5:
+                    scale_rows(5)
+                    weight_columns(5)
+                else:
+                    normalise(rnd - 1)
             if 0 <= m_tile - 1 < TILES:
                 quantise_m(m_tile - 1)
-            for tile, half in ups:
-                add_b1(tile, half)
-                gelu_and_store(tile, half)
-            if 1 < rnd + 1 < TILES:
-                project(rnd + 1)
-            for tile in {5: (7,)}.get(rnd, ()):
-                add_bias_to_x_in_psum(tile)
-            for tile in {0: (2,), 1: (3,), 2: (6,)}.get(rnd, ()):
-                add_bias_to_x(tile)
+            if 0 <= up < TILES:
+                gelu_and_store(up, 0)
+                add_b1(up, 1)
+            if 1 <= rnd <= unit_rounds:
+                for i in (2 * rnd - 2, 2 * rnd - 1):
+                    quantise_unit(units[i], grouped[i])
+            if 0 <= m_tile < TILES:
+                copy_out_m(m_tile)
+            if 0 <= up < TILES:
+                gelu_and_store(up, 1)
+            if now:
+                grouped[now[1]] = new_grouped(now[1] + 6)
+                copy_out_unit(banks[now[1]], grouped[now[1]], units[now[1]][3])

@@ -88,16 +88,16 @@ def tile_transformerblock_pb_kernel(
         load_vector(0, BO_ROWS, out_proj_b)
         load_vector(BO_ROWS, W2_ROWS, w_norm2)
         load_vector(BO_ROWS + W2_ROWS, B1_ROWS, b1)
-        load_heads(0, (0,))
-        load_x(0)
-        load_heads(0, (1,))
         load_weight(wo_raw, "wo_raw", out_proj_w, 0)
+        load_x(0)
+        load_heads(0)
         load_weight(wo_raw, "wo_raw", out_proj_w, 1)
         load_x(1)
         load_heads(1)
         load_x(2)
+        load_weight(w1_raw, "w1_raw", W1, 0)
         load_x(3)
-        for chunk in range(FF // BANK):
+        for chunk in range(1, FF // BANK):
             load_weight(w1_raw, "w1_raw", W1, chunk)
 
         c_words = keep.tile([P, BATCH, PASSES, POS, P], U32, align_bytes=256)
@@ -152,14 +152,14 @@ def tile_transformerblock_pb_kernel(
             )
 
         def transpose_half(unit, half, i):
-            bank = psum.tile([P, 2, HALVES, P], F32, tag="bank", name="unit_%d_%d" % (i, half))
+            bank = psum.tile([P, 2, HALVES, P], F32, tag="bank", name="unit_%s_%d" % (i, half))
             for k in range(2):
                 for u in range(HALVES):
                     nc.tensor.transpose(bank[:, k, u, :], unit[0][2 * half + k][:, u::HALVES], ident_f32[:])
             return bank
 
         def new_grouped(i):
-            return stream.tile([P, PACK * BANK], BF16, align_bytes=64, name="grouped_%d" % i, tag="grouped", bufs=2 * UNITS_PER_ROUND)
+            return stream.tile([P, PACK * BANK], BF16, align_bytes=64, name="grouped_%s" % i, tag="grouped", bufs=2 * UNITS_PER_ROUND)
 
         def copy_out_half(banks, grouped, rows_are_tokens, half, copy):
             blocks = slice(2 * half, 2 * half + 2)
@@ -181,18 +181,6 @@ def tile_transformerblock_pb_kernel(
             nc.vector.tensor_tensor(
                 out=x1_tiles[tile][:], in0=x_raw[j][:, b * DIM : (b + 1) * DIM], in1=bo_all, op=ALU.add
             )
-
-        def add_bias_to_x_on_gpsimd(tile):
-            b, j = divmod(tile, POS)
-            x1_tiles[tile] = keep.tile([P, DIM], F32, name="x1_%d" % tile)
-            for n in range(DIM // BANK):
-                cols = slice(n * BANK, (n + 1) * BANK)
-                nc.gpsimd.tensor_tensor(
-                    out=x1_tiles[tile][:, cols],
-                    in0=x_raw[j][:, b * DIM + n * BANK : b * DIM + (n + 1) * BANK],
-                    in1=bo_all[:, cols],
-                    op=ALU.add,
-                )
 
         xb_banks = {}
 
@@ -276,21 +264,6 @@ def tile_transformerblock_pb_kernel(
                     op1=ALU.mult,
                 )
 
-        n_tiles = {}
-
-        def scale_rows(tile):
-            n_tiles[tile] = stream.tile([P, DIM], F32, name="n_%d" % tile, tag="n", bufs=1)
-            nc.scalar.activation(out=n_tiles[tile][:], in_=x1_tiles[tile][:], func=ACT.Copy, scale=inv_rms[:, tile : tile + 1])
-
-        def weight_columns(tile):
-            m_tiles[tile] = stream.tile([P, HALVES, DIM // PACK, 2], BF16, name="m_%d" % tile, tag="m", bufs=2)
-            n_halves = n_tiles[tile][:].rearrange("p (q u e) -> p u q e", u=HALVES, e=2)
-            w2_halves = w2_all.rearrange("p (q u e) -> p u q e", u=HALVES, e=2)
-            for u in range(HALVES):
-                nc.gpsimd.tensor_tensor(
-                    out=m_tiles[tile][:, u, :, :], in0=n_halves[:, u, :, :], in1=w2_halves[:, u, :, :], op=ALU.mult
-                )
-
         m_banks = {}
 
         def transpose_m(tile):
@@ -358,100 +331,99 @@ def tile_transformerblock_pb_kernel(
                 out=out1_view[:, j, b, half * FF // 2 : (half + 1) * FF // 2], in_=g_tiles[tile, half][:]
             )
 
-        def transpose_unit(unit, i):
-            return [transpose_half(unit, half, i) for half in range(2)]
+        token_units = [token_unit(0, g) for g in range(PASSES)]
+        wo_units = [weight_unit(wo_raw, wo_words, wo_scales, chunk, g) for chunk in range(2) for g in range(PASSES)]
+        head_units = wo_units[:2] + token_units + wo_units[2:]
+        head_banks, head_grouped = {}, {}
 
-        def copy_out_unit(banks, grouped, rows_are_tokens, copies=(nc.scalar.copy, nc.scalar.copy)):
-            for half in range(2):
-                copy_out_half(banks, grouped, rows_are_tokens, half, copies[half])
+        def transpose_unit(unit, name):
+            return [transpose_half(unit, half, name) for half in range(2)]
 
-        for first in range(0, 8, 2):
-            spread_matmuls(first)
-        for first in range(0, 8, 2):
-            copy_out_spread(first, nc.vector.tensor_copy if first % 4 == 0 else nc.scalar.copy)
-        add_bias_to_x_on_gpsimd(0)
-        add_bias_to_x_on_gpsimd(4)
-        head_units = [token_unit(0, q) for q in range(PASSES)]
-        head_units += [weight_unit(wo_raw, wo_words, wo_scales, chunk, q) for chunk in range(2) for q in range(PASSES)]
-        head_grouped = {}
-        for i in range(2):
-            banks = transpose_unit(head_units[i], i)
-            head_grouped[i] = new_grouped(i)
-            copy_out_unit(banks, head_grouped[i], True, (nc.vector.tensor_copy, nc.scalar.copy))
-        quantise_unit(head_units[0], head_grouped[0])
-        quantise_unit(head_units[1], head_grouped[1])
-        for i in range(2, 6):
-            banks = transpose_unit(head_units[i], i)
-            head_grouped[i] = new_grouped(i)
-            copy_out_unit(banks, head_grouped[i], False)
-            if i == 3:
-                add_bias_to_x(5)
-            if i == 5:
+        def copy_out_unit(banks, unit, name, first_copy=nc.scalar.copy):
+            grouped = new_grouped(name)
+            copy_out_half(banks, grouped, unit[3], 0, first_copy)
+            copy_out_half(banks, grouped, unit[3], 1, nc.scalar.copy)
+            return grouped
+
+        spread_matmuls(0)
+        spread_matmuls(2)
+        spread_matmuls(4)
+        copy_out_spread(0, nc.vector.tensor_copy)
+        copy_out_spread(2, nc.scalar.copy)
+        copy_out_spread(4, nc.vector.tensor_copy)
+        add_bias_to_x(0)
+        add_bias_to_x(4)
+        for i, unit in enumerate(head_units):
+            if i == 2:
+                spread_matmuls(6)
+                copy_out_spread(6, nc.scalar.copy)
+            banks = transpose_unit(unit, i)
+            head_grouped[i] = copy_out_unit(banks, unit, i, nc.vector.tensor_copy if i == 2 else nc.scalar.copy)
+            if i == 2:
+                quantise_unit(head_units[1], head_grouped[1])
+            elif i == 4:
+                quantise_unit(head_units[2], head_grouped[2])
+                quantise_unit(head_units[3], head_grouped[3])
                 add_bias_to_x(1)
-            quantise_unit(head_units[i], head_grouped[i])
+                quantise_unit(unit, head_grouped[i])
+            elif i == 5:
+                quantise_unit(unit, head_grouped[i])
+                add_bias_to_x(5)
+            elif i == 0:
+                quantise_unit(unit, head_grouped[i])
 
-        units = [token_unit(1, q) for q in range(PASSES)]
-        units += [weight_unit(w1_raw, w1_words, w1_scales, chunk, q) for chunk in range(4) for q in range(PASSES)]
-        unit_rounds = 5
+        units = [token_unit(1, g) for g in range(PASSES)]
+        units += [weight_unit(w1_raw, w1_words, w1_scales, chunk, g) for chunk in range(FF // BANK) for g in range(PASSES)]
+        unit_rounds = len(units) // 2
+        up_lag = 7
         grouped = {}
-        for rnd in range(6 + TILES):
-            now = (2 * rnd, 2 * rnd + 1) if rnd < unit_rounds else ()
-            up = rnd - 6
+        for rnd in range(up_lag + TILES):
+            up = rnd - up_lag
             m_tile = rnd - 2
-            banks = {}
-            if 0 <= up < TILES:
-                up_project(up, 0)
-            if 1 < rnd + 1 < TILES:
-                project(rnd + 1, (0,))
-            if rnd == 5:
-                sum_bias_and_x(6)
+            first, second = 2 * rnd, 2 * rnd + 1
+            if rnd < unit_rounds:
+                banks = transpose_unit(units[first], "a%d" % rnd)
+                grouped[first] = copy_out_unit(banks, units[first], "a%d" % rnd)
             if rnd == 0:
-                banks[0] = transpose_unit(units[0], 6)
                 project(0)
                 project(1)
+            if 0 <= up:
+                up_project(up, 0)
             if rnd < TILES:
                 add_residual(rnd)
-            for tile in {1: (2, 7)}.get(rnd, ()):
-                add_bias_to_x(tile)
-            for tile in {0: (3,)}.get(rnd, ()):
-                add_bias_to_x_on_gpsimd(tile)
-            if 0 <= up < TILES:
+            if 1 <= rnd < TILES - 1:
+                project(rnd + 1, (0,))
+            if 0 <= up:
                 add_b1(up, 0)
-                up_project(up, 1)
-            if now and rnd:
-                banks[now[0]] = transpose_unit(units[now[0]], now[0] + 6)
-            if now:
-                grouped[now[0]] = new_grouped(now[0] + 6)
-                copy_out_unit(banks[now[0]], grouped[now[0]], units[now[0]][3])
-            if rnd == 5:
-                copy_out_bias_and_x(6)
+                gelu_and_store(up, 0)
+            if rnd < unit_rounds:
+                banks = transpose_unit(units[second], "b%d" % rnd)
             if rnd < TILES:
                 sum_squares(rnd)
                 inverse_rms(rnd)
-            if 1 < rnd + 1 < TILES:
+            if rnd < unit_rounds:
+                grouped[second] = copy_out_unit(banks, units[second], "b%d" % rnd)
+            if 1 <= rnd < TILES - 1:
                 project(rnd + 1, (1,))
+            if rnd == 1:
+                add_bias_to_x(2)
+                add_bias_to_x(3)
+            if 0 <= up:
+                up_project(up, 1)
+                add_b1(up, 1)
             if 0 <= m_tile < TILES:
                 transpose_m(m_tile)
-            if now:
-                banks[now[1]] = transpose_unit(units[now[1]], now[1] + 6)
             if 1 <= rnd <= TILES:
-                if rnd - 1 == 5:
-                    scale_rows(5)
-                    weight_columns(5)
-                else:
-                    normalise(rnd - 1)
+                normalise(rnd - 1)
             if 0 <= m_tile - 1 < TILES:
                 quantise_m(m_tile - 1)
-            if 0 <= up < TILES:
-                gelu_and_store(up, 0)
-                add_b1(up, 1)
-            if 1 <= rnd <= unit_rounds:
-                for i in (2 * rnd - 2, 2 * rnd - 1):
-                    quantise_unit(units[i], grouped[i])
             if 0 <= m_tile < TILES:
                 copy_out_m(m_tile)
-            if 0 <= up < TILES:
+            if rnd in (4, 5):
+                sum_bias_and_x(rnd + 2)
+                copy_out_bias_and_x(rnd + 2)
+            if 0 <= up:
                 gelu_and_store(up, 1)
-            if now:
-                grouped[now[1]] = new_grouped(now[1] + 6)
-                copy_out_unit(banks[now[1]], grouped[now[1]], units[now[1]][3])
+            if 1 <= rnd <= unit_rounds:
+                quantise_unit(units[first - 2], grouped[first - 2])
+                quantise_unit(units[second - 2], grouped[second - 2])

@@ -48,10 +48,10 @@ def tile_transformerblock_pb_kernel(
         nc.vector.memset(table_warmer[:], 0.0)
         minus_half = const.tile([P, 1], F32)
         nc.vector.memset(minus_half[:], -0.5)
-        ident_bf16 = const.tile([P, P], BF16)
-        make_identity(nc, ident_bf16[:])
         ident_f32 = const.tile([P, P], F32)
         make_identity(nc, ident_f32[:])
+        ident_bf16 = const.tile([P, P], BF16)
+        make_identity(nc, ident_bf16[:])
         nc.scalar.activation(out=table_warmer[:], in_=table_warmer[:], func=ACT.Gelu)
 
         x_view = x.rearrange("(p j) b d -> p j (b d)", j=POS)
@@ -85,19 +85,18 @@ def tile_transformerblock_pb_kernel(
                 in_=weight[chunk * BANK : (chunk + 1) * BANK, :].rearrange("(p a) k -> p (a k)", a=PACK),
             )
 
+        load_heads(0)
         load_vector(0, BO_ROWS, out_proj_b)
         load_vector(BO_ROWS, W2_ROWS, w_norm2)
         load_vector(BO_ROWS + W2_ROWS, B1_ROWS, b1)
         load_weight(wo_raw, "wo_raw", out_proj_w, 0)
         load_x(0)
-        load_heads(0)
         load_weight(wo_raw, "wo_raw", out_proj_w, 1)
         load_x(1)
         load_heads(1)
         load_x(2)
-        load_weight(w1_raw, "w1_raw", W1, 0)
         load_x(3)
-        for chunk in range(1, FF // BANK):
+        for chunk in range(FF // BANK):
             load_weight(w1_raw, "w1_raw", W1, chunk)
 
         c_words = keep.tile([P, BATCH, PASSES, POS, P], U32, align_bytes=256)
@@ -331,99 +330,97 @@ def tile_transformerblock_pb_kernel(
                 out=out1_view[:, j, b, half * FF // 2 : (half + 1) * FF // 2], in_=g_tiles[tile, half][:]
             )
 
-        token_units = [token_unit(0, g) for g in range(PASSES)]
-        wo_units = [weight_unit(wo_raw, wo_words, wo_scales, chunk, g) for chunk in range(2) for g in range(PASSES)]
-        head_units = wo_units[:2] + token_units + wo_units[2:]
-        head_banks, head_grouped = {}, {}
+        head_units = [token_unit(0, g) for g in range(PASSES)]
+        head_units += [weight_unit(wo_raw, wo_words, wo_scales, chunk, g) for chunk in range(2) for g in range(PASSES)]
+        head_grouped = {}
 
         def transpose_unit(unit, name):
             return [transpose_half(unit, half, name) for half in range(2)]
 
-        def copy_out_unit(banks, unit, name, first_copy=nc.scalar.copy):
+        def copy_out_unit(banks, unit, name):
             grouped = new_grouped(name)
-            copy_out_half(banks, grouped, unit[3], 0, first_copy)
+            copy_out_half(banks, grouped, unit[3], 0, nc.scalar.copy)
             copy_out_half(banks, grouped, unit[3], 1, nc.scalar.copy)
             return grouped
 
-        spread_matmuls(0)
-        spread_matmuls(2)
-        spread_matmuls(4)
-        copy_out_spread(0, nc.vector.tensor_copy)
-        copy_out_spread(2, nc.scalar.copy)
-        copy_out_spread(4, nc.vector.tensor_copy)
+        def prepare(i):
+            head_grouped[i] = copy_out_unit(transpose_unit(head_units[i], i), head_units[i], i)
+
+        prepare(0)
+        prepare(1)
+        for first in (0, 2, 4):
+            spread_matmuls(first)
+            copy_out_spread(first, nc.scalar.copy)
+        quantise_unit(head_units[0], head_grouped[0])
         add_bias_to_x(0)
+        prepare(2)
         add_bias_to_x(4)
-        for i, unit in enumerate(head_units):
-            if i == 2:
-                spread_matmuls(6)
-                copy_out_spread(6, nc.scalar.copy)
-            banks = transpose_unit(unit, i)
-            head_grouped[i] = copy_out_unit(banks, unit, i, nc.vector.tensor_copy if i == 2 else nc.scalar.copy)
-            if i == 2:
-                quantise_unit(head_units[1], head_grouped[1])
-            elif i == 4:
-                quantise_unit(head_units[2], head_grouped[2])
-                quantise_unit(head_units[3], head_grouped[3])
-                add_bias_to_x(1)
-                quantise_unit(unit, head_grouped[i])
-            elif i == 5:
-                quantise_unit(unit, head_grouped[i])
-                add_bias_to_x(5)
-            elif i == 0:
-                quantise_unit(unit, head_grouped[i])
+        quantise_unit(head_units[1], head_grouped[1])
+        prepare(3)
+        quantise_unit(head_units[2], head_grouped[2])
+        prepare(4)
+        add_bias_to_x(1)
+        quantise_unit(head_units[3], head_grouped[3])
+        prepare(5)
+        spread_matmuls(6)
+        copy_out_spread(6, nc.scalar.copy)
+        quantise_unit(head_units[4], head_grouped[4])
+        quantise_unit(head_units[5], head_grouped[5])
+        add_bias_to_x(5)
 
         units = [token_unit(1, g) for g in range(PASSES)]
         units += [weight_unit(w1_raw, w1_words, w1_scales, chunk, g) for chunk in range(FF // BANK) for g in range(PASSES)]
         unit_rounds = len(units) // 2
-        up_lag = 7
+        up_lag = unit_rounds + 1
         grouped = {}
         for rnd in range(up_lag + TILES):
             up = rnd - up_lag
             m_tile = rnd - 2
             first, second = 2 * rnd, 2 * rnd + 1
+            if 0 <= up:
+                up_project(up, 0)
             if rnd < unit_rounds:
                 banks = transpose_unit(units[first], "a%d" % rnd)
                 grouped[first] = copy_out_unit(banks, units[first], "a%d" % rnd)
             if rnd == 0:
                 project(0)
                 project(1)
-            if 0 <= up:
-                up_project(up, 0)
             if rnd < TILES:
                 add_residual(rnd)
             if 1 <= rnd < TILES - 1:
                 project(rnd + 1, (0,))
-            if 0 <= up:
-                add_b1(up, 0)
-                gelu_and_store(up, 0)
-            if rnd < unit_rounds:
-                banks = transpose_unit(units[second], "b%d" % rnd)
-            if rnd < TILES:
-                sum_squares(rnd)
-                inverse_rms(rnd)
-            if rnd < unit_rounds:
-                grouped[second] = copy_out_unit(banks, units[second], "b%d" % rnd)
-            if 1 <= rnd < TILES - 1:
-                project(rnd + 1, (1,))
-            if rnd == 1:
-                add_bias_to_x(2)
-                add_bias_to_x(3)
-            if 0 <= up:
-                up_project(up, 1)
-                add_b1(up, 1)
-            if 0 <= m_tile < TILES:
-                transpose_m(m_tile)
-            if 1 <= rnd <= TILES:
-                normalise(rnd - 1)
-            if 0 <= m_tile - 1 < TILES:
-                quantise_m(m_tile - 1)
-            if 0 <= m_tile < TILES:
-                copy_out_m(m_tile)
-            if rnd in (4, 5):
-                sum_bias_and_x(rnd + 2)
-                copy_out_bias_and_x(rnd + 2)
-            if 0 <= up:
-                gelu_and_store(up, 1)
             if 1 <= rnd <= unit_rounds:
                 quantise_unit(units[first - 2], grouped[first - 2])
                 quantise_unit(units[second - 2], grouped[second - 2])
+            if rnd in (0, 1):
+                add_bias_to_x(rnd + 2)
+            if 1 <= rnd <= TILES:
+                normalise(rnd - 1)
+            if 0 <= up:
+                add_b1(up, 0)
+                up_project(up, 1)
+            if rnd < TILES:
+                sum_squares(rnd)
+                inverse_rms(rnd)
+            if 1 <= rnd < TILES - 1:
+                project(rnd + 1, (1,))
+            if rnd == 5:
+                for tile in (6, 7):
+                    sum_bias_and_x(tile)
+                    copy_out_bias_and_x(tile)
+            if 0 <= up:
+                gelu_and_store(up, 0)
+            if 0 <= m_tile < TILES:
+                transpose_m(m_tile)
+            if rnd < unit_rounds:
+                banks = transpose_unit(units[second], "b%d" % rnd)
+            if 0 <= m_tile - 1 < TILES:
+                quantise_m(m_tile - 1)
+            if 0 <= up:
+                add_b1(up, 1)
+            if 0 <= m_tile < TILES:
+                copy_out_m(m_tile)
+            if 0 <= up:
+                gelu_and_store(up, 1)
+            if rnd < unit_rounds:
+                grouped[second] = copy_out_unit(banks, units[second], "b%d" % rnd)

@@ -348,79 +348,75 @@ def tile_transformerblock_pb_kernel(
 
         prepare(0)
         prepare(1)
-        for first in (0, 2, 4):
-            spread_matmuls(first)
-            copy_out_spread(first, nc.scalar.copy)
         quantise_unit(head_units[0], head_grouped[0])
-        add_bias_to_x(0)
-        prepare(2)
-        add_bias_to_x(4)
+        spread_matmuls(0)
+        spread_matmuls(2)
+        copy_out_spread(0, nc.vector.tensor_copy)
+        copy_out_spread(2, nc.scalar.copy)
         quantise_unit(head_units[1], head_grouped[1])
+        add_bias_to_x(0)
+        add_bias_to_x(4)
+        prepare(2)
         prepare(3)
         quantise_unit(head_units[2], head_grouped[2])
-        prepare(4)
-        add_bias_to_x(1)
         quantise_unit(head_units[3], head_grouped[3])
+        add_bias_to_x(5)
+        prepare(4)
         prepare(5)
-        spread_matmuls(6)
-        copy_out_spread(6, nc.scalar.copy)
+        for first in (4, 6):
+            spread_matmuls(first)
+            copy_out_spread(first, nc.scalar.copy)
         quantise_unit(head_units[4], head_grouped[4])
         quantise_unit(head_units[5], head_grouped[5])
-        add_bias_to_x(5)
+        add_bias_to_x(1)
 
         units = [token_unit(1, g) for g in range(PASSES)]
         units += [weight_unit(w1_raw, w1_words, w1_scales, chunk, g) for chunk in range(FF // BANK) for g in range(PASSES)]
         unit_rounds = len(units) // 2
-        up_lag = unit_rounds + 1
+        up_lag = unit_rounds
         grouped = {}
+        project(0)
         for rnd in range(up_lag + TILES):
             up = rnd - up_lag
-            m_tile = rnd - 2
             first, second = 2 * rnd, 2 * rnd + 1
             if 0 <= up:
                 up_project(up, 0)
-            if rnd < unit_rounds:
-                banks = transpose_unit(units[first], "a%d" % rnd)
-                grouped[first] = copy_out_unit(banks, units[first], "a%d" % rnd)
-            if rnd == 0:
-                project(0)
-                project(1)
             if rnd < TILES:
                 add_residual(rnd)
-            if 1 <= rnd < TILES - 1:
-                project(rnd + 1, (0,))
-            if 1 <= rnd <= unit_rounds:
-                quantise_unit(units[first - 2], grouped[first - 2])
-                quantise_unit(units[second - 2], grouped[second - 2])
-            if rnd in (0, 1):
-                add_bias_to_x(rnd + 2)
+            for tile in {0: (2, 3), 3: (6,)}.get(rnd, ()):
+                add_bias_to_x(tile)
             if 1 <= rnd <= TILES:
                 normalise(rnd - 1)
-            if 0 <= up:
-                add_b1(up, 0)
-                up_project(up, 1)
             if rnd < TILES:
                 sum_squares(rnd)
                 inverse_rms(rnd)
-            if 1 <= rnd < TILES - 1:
-                project(rnd + 1, (1,))
-            if rnd == 5:
-                for tile in (6, 7):
-                    sum_bias_and_x(tile)
-                    copy_out_bias_and_x(tile)
+            if 1 <= rnd <= unit_rounds:
+                quantise_unit(units[first - 2], grouped[first - 2])
+                quantise_unit(units[second - 2], grouped[second - 2])
             if 0 <= up:
-                gelu_and_store(up, 0)
-            if 0 <= m_tile < TILES:
-                transpose_m(m_tile)
+                up_project(up, 1)
+                add_b1(up, 0)
+            if rnd < TILES - 1:
+                project(rnd + 1, (0,))
+            if rnd < unit_rounds:
+                banks = transpose_unit(units[first], "a%d" % rnd)
+                grouped[first] = copy_out_unit(banks, units[first], "a%d" % rnd)
+            if rnd < TILES - 1:
+                project(rnd + 1, (1,))
             if rnd < unit_rounds:
                 banks = transpose_unit(units[second], "b%d" % rnd)
-            if 0 <= m_tile - 1 < TILES:
-                quantise_m(m_tile - 1)
+                grouped[second] = copy_out_unit(banks, units[second], "b%d" % rnd)
             if 0 <= up:
+                gelu_and_store(up, 0)
                 add_b1(up, 1)
-            if 0 <= m_tile < TILES:
-                copy_out_m(m_tile)
+            if 1 <= rnd <= TILES:
+                transpose_m(rnd - 1)
+            if 2 <= rnd <= TILES + 1:
+                quantise_m(rnd - 2)
             if 0 <= up:
                 gelu_and_store(up, 1)
-            if rnd < unit_rounds:
-                grouped[second] = copy_out_unit(banks, units[second], "b%d" % rnd)
+            if rnd == 5:
+                sum_bias_and_x(7)
+                copy_out_bias_and_x(7)
+            if 1 <= rnd <= TILES:
+                copy_out_m(rnd - 1)

@@ -383,7 +383,7 @@ def tile_transformerblock_pb_kernel(
                 up_project(up, 0)
             if rnd < TILES:
                 add_residual(rnd)
-            for tile in {0: (2, 3), 3: (6,)}.get(rnd, ()):
+            for tile in {0: (2, 3)}.get(rnd, ()):
                 add_bias_to_x(tile)
             if 1 <= rnd <= TILES:
                 normalise(rnd - 1)
@@ -415,8 +415,8 @@ def tile_transformerblock_pb_kernel(
                 quantise_m(rnd - 2)
             if 0 <= up:
                 gelu_and_store(up, 1)
-            if rnd == 5:
-                sum_bias_and_x(7)
-                copy_out_bias_and_x(7)
+            if rnd in (4, 5):
+                sum_bias_and_x(rnd + 2)
+                copy_out_bias_and_x(rnd + 2)
             if 1 <= rnd <= TILES:
                 copy_out_m(rnd - 1)

from contextlib import ExitStack

import concourse.mybir as mybir
from concourse.masks import make_identity

BF16 = mybir.dt.bfloat16
F32 = mybir.dt.float32
U32 = mybir.dt.uint32
U8 = mybir.dt.uint8
FP8X4 = mybir.dt.float8_e4m3fn_x4
ALU = mybir.AluOpType
ACT = mybir.ActivationFunctionType

P = 128
PACK = 4
K_PASS = P * PACK
BANK = 512
SEQ, BATCH, DIM, HEADS, FF = 512, 2, 1024, 2, 2048
HEAD_DIM = DIM // HEADS
PASSES = DIM // K_PASS
POS = SEQ // P
TILES = BATCH * POS
PAIRS = K_PASS // 2
HALVES = PAIRS // P
EPS = 1e-8
BO_ROWS, W2_ROWS, B1_ROWS = DIM // BANK, DIM // BANK, FF // BANK
G_BUFS = 8
UNITS_PER_ROUND = 2

FLOPS = 2 * SEQ * BATCH * DIM * (DIM + FF)


def tile_transformerblock_pb_kernel(
    tc, h_attn, x, out_proj_w, out_proj_b, w_norm2, W1, b1, out_0, out_1
):
    nc = tc.nc
    with ExitStack() as stack:
        const = stack.enter_context(tc.tile_pool(name="const", bufs=1))
        raw = stack.enter_context(tc.tile_pool(name="raw", bufs=1))
        keep = stack.enter_context(tc.tile_pool(name="keep", bufs=1))
        stream = stack.enter_context(tc.tile_pool(name="stream", bufs=3))
        psum = stack.enter_context(tc.psum_pool(name="psum", bufs=8))
        stack.enter_context(tc.manual_schedule())

        vector_rows = const.tile([P, BANK], BF16)
        nc.vector.memset(vector_rows[:], 0.0)
        table_warmer = const.tile([P, 1], F32)
        nc.vector.memset(table_warmer[:], 0.0)
        minus_half = const.tile([P, 1], F32)
        nc.vector.memset(minus_half[:], -0.5)
        ident_f32 = const.tile([P, P], F32)
        make_identity(nc, ident_f32[:])
        ident_bf16 = const.tile([P, P], BF16)
        make_identity(nc, ident_bf16[:])
        nc.scalar.activation(out=table_warmer[:], in_=table_warmer[:], func=ACT.Gelu)

        x_view = x.rearrange("(p j) b d -> p j (b d)", j=POS)
        out0_view = out_0.rearrange("(p j) b d -> p j b d", j=POS)
        out1_view = out_1.rearrange("(p j) b f -> p j b f", j=POS)
        c_raw = {}
        x_raw = {}
        wo_raw = {}
        w1_raw = {}

        def load_heads(b, heads=range(HEADS)):
            for head in heads:
                c_raw[b, head] = raw.tile([P, POS * HEAD_DIM], BF16, name="c_raw_%d_%d" % (b, head))
                nc.sync.dma_start(
                    out=c_raw[b, head][:], in_=h_attn[b, head].rearrange("(p j) d -> p (j d)", j=POS)
                )

        def load_x(j):
            x_raw[j] = raw.tile([P, BATCH * DIM], BF16, name="x_raw_%d" % j)
            nc.sync.dma_start(out=x_raw[j][:], in_=x_view[:, j, :])

        def load_vector(first_row, n_rows, vector):
            nc.sync.dma_start(
                out=vector_rows[first_row : first_row + n_rows, :], in_=vector.rearrange("(r n) -> r n", n=BANK)
            )

        def load_weight(store, name, weight, chunk):
            store[chunk] = raw.tile([P, PACK * DIM], BF16, name="%s_%d" % (name, chunk))
            nc.sync.dma_start(
                out=store[chunk][:],
                in_=weight[chunk * BANK : (chunk + 1) * BANK, :].rearrange("(p a) k -> p (a k)", a=PACK),
            )

        load_heads(0)
        load_vector(0, BO_ROWS, out_proj_b)
        load_vector(BO_ROWS, W2_ROWS, w_norm2)
        load_vector(BO_ROWS + W2_ROWS, B1_ROWS, b1)
        load_weight(wo_raw, "wo_raw", out_proj_w, 0)
        load_x(0)
        load_weight(wo_raw, "wo_raw", out_proj_w, 1)
        load_x(1)
        load_heads(1)
        load_x(2)
        load_x(3)
        for chunk in range(FF // BANK):
            load_weight(w1_raw, "w1_raw", W1, chunk)

        c_words = keep.tile([P, BATCH, PASSES, POS, P], U32, align_bytes=256)
        c_scales = keep.tile([P, BATCH, PASSES, POS, P], U8, align_bytes=256)
        m_words = keep.tile([P, TILES, PASSES, P], U32, align_bytes=256)
        m_scales = keep.tile([P, TILES, PASSES, P], U8, align_bytes=256)
        wo_words = keep.tile([P, PASSES, DIM], U32, align_bytes=256)
        wo_scales = keep.tile([P, PASSES, DIM], U8, align_bytes=256)
        w1_words = keep.tile([P, PASSES, FF], U32, align_bytes=256)
        w1_scales = keep.tile([P, PASSES, FF], U8, align_bytes=256)

        spread = const.tile([P, BO_ROWS + W2_ROWS + B1_ROWS, BANK], BF16)
        bo_all = spread[:, 0:BO_ROWS, :].rearrange("p r n -> p (r n)")
        w2_all = spread[:, BO_ROWS : BO_ROWS + W2_ROWS, :].rearrange("p r n -> p (r n)")
        b1_all = spread[:, BO_ROWS + W2_ROWS :, :].rearrange("p r n -> p (r n)")

        spread_banks = {}

        def spread_matmuls(first):
            bank = psum.tile([P, 2, BANK], BF16, tag="bank", name="spread_%d" % first)
            spread_banks[first] = bank
            for i in range(2):
                row = first + i
                nc.tensor.matmul(
                    out=bank[:, i, :],
                    lhsT=ident_bf16[:, row : row + 1].to_broadcast([P, P]),
                    rhs=vector_rows[:],
                    start=True,
                    stop=True,
                )

        def copy_out_spread(first, copy):
            copy(out=spread[:, first : first + 2, :], in_=spread_banks[first][:])

        def token_unit(b, g):
            words = c_raw[b, g][:].bitcast(F32)
            return (
                [words[:, j * PAIRS : (j + 1) * PAIRS] for j in range(POS)],
                c_words[:, b, g, :, :].rearrange("p j r -> p (j r)"),
                c_scales[:, b, g, :, :].rearrange("p j r -> p (j r)"),
                True,
            )

        def weight_unit(w_raw, w_words, w_scales, chunk, g):
            words = w_raw[chunk][:].bitcast(F32)
            cols = slice(chunk * BANK, (chunk + 1) * BANK)
            return (
                [words[:, (a * PASSES + g) * PAIRS : (a * PASSES + g + 1) * PAIRS] for a in range(PACK)],
                w_words[:, g, cols],
                w_scales[:, g, cols],
                False,
            )

        def transpose_half(unit, half, i):
            bank = psum.tile([P, 2, HALVES, P], F32, tag="bank", name="unit_%s_%d" % (i, half))
            for k in range(2):
                for u in range(HALVES):
                    nc.tensor.transpose(bank[:, k, u, :], unit[0][2 * half + k][:, u::HALVES], ident_f32[:])
            return bank

        def new_grouped(i):
            return stream.tile([P, PACK * BANK], BF16, align_bytes=64, name="grouped_%s" % i, tag="grouped", bufs=2 * UNITS_PER_ROUND)

        def copy_out_half(banks, grouped, rows_are_tokens, half, copy):
            blocks = slice(2 * half, 2 * half + 2)
            if rows_are_tokens:
                words = grouped[:].bitcast(F32).rearrange("p (i r u) -> p i r u", i=PACK, u=HALVES)
                copy(out=words[:, blocks, :, :], in_=banks[half][:].rearrange("p i u r -> p i r u"))
            else:
                words = grouped[:].bitcast(F32).rearrange("p (r i u) -> p r i u", i=PACK, u=HALVES)
                copy(out=words[:, :, blocks, :], in_=banks[half][:].rearrange("p i u r -> p r i u"))

        def quantise_unit(unit, grouped):
            nc.vector.quantize_mx(out=unit[1].bitcast(FP8X4), scales=unit[2], in_=grouped[:])

        x1_tiles = {}

        def add_bias_to_x(tile):
            b, j = divmod(tile, POS)
            x1_tiles[tile] = keep.tile([P, DIM], F32, name="x1_%d" % tile)
            nc.vector.tensor_tensor(
                out=x1_tiles[tile][:], in0=x_raw[j][:, b * DIM : (b + 1) * DIM], in1=bo_all, op=ALU.add
            )

        xb_banks = {}

        def sum_bias_and_x(tile):
            b, j = divmod(tile, POS)
            x1_tiles[tile] = keep.tile([P, DIM], F32, name="x1_%d" % tile)
            for n in range(DIM // BANK):
                bank = psum.tile([P, BANK], F32, tag="bank", name="xb_%d_%d" % (tile, n))
                xb_banks[tile, n] = bank
                cols = slice(b * DIM + n * BANK, b * DIM + (n + 1) * BANK)
                nc.tensor.matmul(out=bank[:], lhsT=ident_bf16[:], rhs=x_raw[j][:, cols], start=True, stop=False)
                nc.tensor.matmul(
                    out=bank[:],
                    lhsT=ident_bf16[:, n : n + 1].to_broadcast([P, P]),
                    rhs=vector_rows[:],
                    start=False,
                    stop=True,
                )

        def copy_out_bias_and_x(tile):
            for n in range(DIM // BANK):
                nc.scalar.copy(out=x1_tiles[tile][:, n * BANK : (n + 1) * BANK], in_=xb_banks[tile, n][:])

        attn_banks = {}

        def project(tile, halves=range(DIM // BANK)):
            b, j = divmod(tile, POS)
            for n in halves:
                cols = slice(n * BANK, (n + 1) * BANK)
                attn_banks[tile, n] = psum.tile([P, BANK], F32, tag="bank", name="attn_%d_%d" % (tile, n))
                for g in range(PASSES):
                    nc.tensor.matmul_mx(
                        out=attn_banks[tile, n][:],
                        lhsT=c_words[:, b, g, j, :].bitcast(FP8X4),
                        lhsT_scale=c_scales[:, b, g, j, :],
                        rhs=wo_words[:, g, cols].bitcast(FP8X4),
                        rhs_scale=wo_scales[:, g, cols],
                        start=(g == 0),
                        stop=(g == PASSES - 1),
                    )

        def add_residual(tile):
            b, j = divmod(tile, POS)
            x1 = x1_tiles[tile]
            for n in range(DIM // BANK):
                cols = slice(n * BANK, (n + 1) * BANK)
                nc.vector.tensor_tensor(out=x1[:, cols], in0=attn_banks[tile, n][:], in1=x1[:, cols], op=ALU.add)
            nc.sync.dma_start(out=out0_view[:, j, b, :], in_=x1[:])

        mean_sq = const.tile([P, TILES], F32)
        mean_sq_eps = const.tile([P, TILES], F32)
        inv_rms = const.tile([P, TILES], F32)

        def sum_squares(tile):
            col = slice(tile, tile + 1)
            squares = stream.tile([P, DIM], BF16, bufs=2)
            nc.scalar.activation(
                out=squares[:], in_=x1_tiles[tile][:], func=ACT.Square, scale=DIM**-0.5, accum_out=mean_sq[:, col]
            )

        def inverse_rms(tile):
            col = slice(tile, tile + 1)
            nc.gpsimd.tensor_scalar(
                out=mean_sq_eps[:, col], in0=mean_sq[:, col], scalar1=EPS, scalar2=1.0, op0=ALU.add, op1=ALU.mult
            )
            nc.gpsimd.tensor_tensor(out=inv_rms[:, col], in0=mean_sq_eps[:, col], in1=minus_half[:], op=ALU.pow)

        m_tiles = {}

        def normalise(tile):
            m_tiles[tile] = stream.tile([P, HALVES, DIM // PACK, 2], BF16, name="m_%d" % tile, tag="m", bufs=2)
            x1_halves = x1_tiles[tile][:].rearrange("p (q u e) -> p u q e", u=HALVES, e=2)
            w2_halves = w2_all.rearrange("p (q u e) -> p u q e", u=HALVES, e=2)
            for u in range(HALVES):
                nc.vector.scalar_tensor_tensor(
                    out=m_tiles[tile][:, u, :, :],
                    in0=x1_halves[:, u, :, :],
                    scalar=inv_rms[:, tile : tile + 1],
                    in1=w2_halves[:, u, :, :],
                    op0=ALU.mult,
                    op1=ALU.mult,
                )

        m_banks = {}

        def transpose_m(tile):
            m_banks[tile] = psum.tile([P, PASSES, HALVES, P], F32, tag="bank", name="m_bank_%d" % tile)
            words = m_tiles[tile][:].rearrange("p u q e -> p (u q e)").bitcast(F32)
            for g in range(PASSES):
                for u in range(HALVES):
                    first = (u * PASSES + g) * P
                    nc.tensor.transpose(m_banks[tile][:, g, u, :], words[:, first : first + P], ident_f32[:])

        grouped_m = {}

        def copy_out_m(tile):
            grouped_m[tile] = stream.tile(
                [P, PASSES * P * PACK], BF16, align_bytes=64, name="grouped_m_%d" % tile, tag="grouped_m", bufs=2
            )
            nc.scalar.copy(
                out=grouped_m[tile][:].bitcast(F32).rearrange("p (g r u) -> p g r u", g=PASSES, u=HALVES),
                in_=m_banks[tile][:].rearrange("p g u r -> p g r u"),
            )

        def quantise_m(tile):
            nc.vector.quantize_mx(
                out=m_words[:, tile, :, :].rearrange("p g r -> p (g r)").bitcast(FP8X4),
                scales=m_scales[:, tile, :, :].rearrange("p g r -> p (g r)"),
                in_=grouped_m[tile][:],
            )

        up_banks = {}

        def up_project(tile, half):
            for n in (2 * half, 2 * half + 1):
                cols = slice(n * BANK, (n + 1) * BANK)
                up_banks[tile, n] = psum.tile([P, BANK], F32, tag="bank", name="up_%d_%d" % (tile, n))
                for g in range(PASSES):
                    nc.tensor.matmul_mx(
                        out=up_banks[tile, n][:],
                        lhsT=m_words[:, tile, g, :].bitcast(FP8X4),
                        lhsT_scale=m_scales[:, tile, g, :],
                        rhs=w1_words[:, g, cols].bitcast(FP8X4),
                        rhs_scale=w1_scales[:, g, cols],
                        start=(g == 0),
                        stop=(g == PASSES - 1),
                    )

        g_tiles = {}

        def add_b1(tile, half):
            g_tiles[tile, half] = stream.tile([P, FF // 2], F32, name="g_%d_%d" % (tile, half), tag="g", bufs=G_BUFS)
            for i in range(2):
                n = 2 * half + i
                nc.vector.tensor_tensor(
                    out=g_tiles[tile, half][:, i * BANK : (i + 1) * BANK],
                    in0=up_banks[tile, n][:],
                    in1=b1_all[:, n * BANK : (n + 1) * BANK],
                    op=ALU.add,
                )

        def gelu_and_store(tile, half):
            b, j = divmod(tile, POS)
            for i in range(2):
                cols = slice(i * BANK, (i + 1) * BANK)
                nc.scalar.activation(out=g_tiles[tile, half][:, cols], in_=g_tiles[tile, half][:, cols], func=ACT.Gelu)
            nc.sync.dma_start(
                out=out1_view[:, j, b, half * FF // 2 : (half + 1) * FF // 2], in_=g_tiles[tile, half][:]
            )

        head_units = [token_unit(0, g) for g in range(PASSES)]
        head_units += [weight_unit(wo_raw, wo_words, wo_scales, chunk, g) for chunk in range(2) for g in range(PASSES)]
        head_grouped = {}

        def transpose_unit(unit, name):
            return [transpose_half(unit, half, name) for half in range(2)]

        def copy_out_unit(banks, unit, name):
            grouped = new_grouped(name)
            copy_out_half(banks, grouped, unit[3], 0, nc.scalar.copy)
            copy_out_half(banks, grouped, unit[3], 1, nc.scalar.copy)
            return grouped

        def prepare(i):
            head_grouped[i] = copy_out_unit(transpose_unit(head_units[i], i), head_units[i], i)

        prepare(0)
        prepare(1)
        quantise_unit(head_units[0], head_grouped[0])
        spread_matmuls(0)
        spread_matmuls(2)
        copy_out_spread(0, nc.vector.tensor_copy)
        copy_out_spread(2, nc.scalar.copy)
        quantise_unit(head_units[1], head_grouped[1])
        add_bias_to_x(0)
        add_bias_to_x(4)
        prepare(2)
        prepare(3)
        quantise_unit(head_units[2], head_grouped[2])
        quantise_unit(head_units[3], head_grouped[3])
        add_bias_to_x(5)
        prepare(4)
        prepare(5)
        for first in (4, 6):
            spread_matmuls(first)
            copy_out_spread(first, nc.scalar.copy)
        quantise_unit(head_units[4], head_grouped[4])
        quantise_unit(head_units[5], head_grouped[5])
        add_bias_to_x(1)

        units = [token_unit(1, g) for g in range(PASSES)]
        units += [weight_unit(w1_raw, w1_words, w1_scales, chunk, g) for chunk in range(FF // BANK) for g in range(PASSES)]
        unit_rounds = len(units) // 2
        up_lag = unit_rounds
        grouped = {}
        project(0)
        for rnd in range(up_lag + TILES):
            up = rnd - up_lag
            first, second = 2 * rnd, 2 * rnd + 1
            if 0 <= up:
                up_project(up, 0)
            if rnd < TILES:
                add_residual(rnd)
            for tile in {0: (2, 3)}.get(rnd, ()):
                add_bias_to_x(tile)
            if 1 <= rnd <= TILES:
                normalise(rnd - 1)
            if rnd < TILES:
                sum_squares(rnd)
                inverse_rms(rnd)
            if 1 <= rnd <= unit_rounds:
                quantise_unit(units[first - 2], grouped[first - 2])
                quantise_unit(units[second - 2], grouped[second - 2])
            if 0 <= up:
                up_project(up, 1)
                add_b1(up, 0)
            if rnd < TILES - 1:
                project(rnd + 1, (0,))
            if rnd < unit_rounds:
                banks = transpose_unit(units[first], "a%d" % rnd)
                grouped[first] = copy_out_unit(banks, units[first], "a%d" % rnd)
            if rnd < TILES - 1:
                project(rnd + 1, (1,))
            if rnd < unit_rounds:
                banks = transpose_unit(units[second], "b%d" % rnd)
                grouped[second] = copy_out_unit(banks, units[second], "b%d" % rnd)
            if 0 <= up:
                gelu_and_store(up, 0)
                add_b1(up, 1)
            if 1 <= rnd <= TILES:
                transpose_m(rnd - 1)
            if 2 <= rnd <= TILES + 1:
                quantise_m(rnd - 2)
            if 0 <= up:
                gelu_and_store(up, 1)
            if rnd in (4, 5):
                sum_bias_and_x(rnd + 2)
                copy_out_bias_and_x(rnd + 2)
            if 1 <= rnd <= TILES:
                copy_out_m(rnd - 1)
